import numpy as np
import ml_dtypes


def mxq(x, axis, fmt="e4m3"):
    dtype, down = {"e4m3": (ml_dtypes.float8_e4m3fn, 7), "e5m2": (ml_dtypes.float8_e5m2, 14)}[fmt]
    v = np.moveaxis(np.asarray(x, np.float32).astype(ml_dtypes.bfloat16).astype(np.float64), axis, -1)
    blocks = v.reshape(v.shape[:-1] + (-1, 32))
    amax = np.abs(blocks).max(-1, keepdims=True)
    byte = np.maximum(np.where(amax > 0, np.frexp(amax)[1] - 1 + 127, 0) - down, 1)
    scale = np.exp2(byte - 127.0)
    codes = (blocks / scale).astype(np.float32).astype(dtype).astype(np.float64)
    return np.moveaxis((codes * scale).reshape(v.shape), -1, axis)


WIDE = False


def mx_kscale(k):
    if not WIDE:
        return np.ones(k)
    levels = np.array([20, -20, 10, -10, 0])
    a = np.random.permutation(np.resize(levels, k // 512 * 4)).reshape(k // 512, 4)
    idx = np.arange(k)
    return np.exp2(a[idx // 512, idx % 128 // 32])


BF16 = ml_dtypes.bfloat16


def bf(x):
    return np.asarray(x, np.float32).astype(BF16)


def f64(x):
    return np.asarray(x).astype(np.float64)


B, I, H, P = 4096, 256, 512, 2048
C = I + H


def sigmoid(v):
    return 1.0 / (1.0 + np.exp(-v))


def setup_inputs():
    s = mx_kscale(B)[:, None]
    x = np.random.standard_normal((B, I)) * s
    rh = np.random.standard_normal((B, H)) * 0.95 * s
    update = np.random.standard_normal((B, H)) * 0.7
    hidden = 1.5 + np.random.standard_normal((B, H))
    Wn = np.random.standard_normal((H, C)) / np.sqrt(C)
    bn = -0.1 + 0.2 * np.random.standard_normal(H)
    connection_strength = 1.0 + 0.3 * np.random.standard_normal(H)
    connection_decay = 0.4 + 0.2 * np.random.random(1)
    connection_history = 2.0 * np.random.standard_normal(H)
    g = np.random.standard_normal((B, H)) * np.exp2(np.random.randint(-12, 1, (B, 1))) / s
    return {"x": bf(x),
            "rh": bf(rh),
            "update": bf(update),
            "hidden": bf(hidden),
            "Wn": bf(Wn),
            "bn": bf(bn),
            "connection_strength": bf(connection_strength),
            "connection_decay": bf(connection_decay),
            "connection_history": bf(connection_history),
            "grad_out": bf(g)}


def reference(x, rh, update, hidden, Wn, bn, connection_strength, connection_decay, connection_history, grad_out):
    h = f64(hidden)
    activity = np.mean(np.abs(h), axis=0)
    ch = f64(connection_history) * f64(connection_decay) + activity
    cs = f64(connection_strength) * sigmoid(ch)
    gu = f64(grad_out) * f64(update)
    combined_reset = np.concatenate([f64(x), f64(rh)], axis=1)
    prod = mxq(gu, 0, "e5m2").T @ mxq(combined_reset, 0, "e4m3")
    return cs[:, None] * prod

@@ -1,0 +1,201 @@
+from contextlib import ExitStack
+
+import concourse.mybir as mybir
+from concourse.masks import make_identity
+
+F32 = mybir.dt.float32
+BF16 = mybir.dt.bfloat16
+U32 = mybir.dt.uint32
+U8 = mybir.dt.uint8
+E4M3_X4 = mybir.dt.float8_e4m3fn_x4
+E5M2_X4 = mybir.dt.float8_e5m2_x4
+ALU = mybir.AluOpType
+ACT = mybir.ActivationFunctionType
+
+B, I, H = 4096, 256, 512
+C = I + H
+P = 128
+PACK = 4
+K_PASS = P * PACK
+PASSES = B // K_PASS
+M_TILES = H // P
+N_PASS = 512
+HID_CHUNKS = 4
+HID_ROWS = B // P // HID_CHUNKS
+
+FLOPS = 2 * B * H * C
+BYTES = 2 * (B * I + 4 * B * H + 2 * H + 1) + 4 * H * C
+
+
+def regroup(copy, grouped, rows):
+    copy(
+        out=grouped.rearrange("p (c i) t -> p c t i", i=4),
+        in_=rows.rearrange("p t (c i) -> p c t i", i=4),
+    )
+
+
+def tile_persistentgrucell_pb_t_kernel(
+    tc,
+    x,
+    rh,
+    update,
+    hidden,
+    Wn,
+    bn,
+    connection_strength,
+    connection_decay,
+    connection_history,
+    grad_out,
+    out,
+):
+    nc = tc.nc
+    with ExitStack() as ctx:
+        consts = ctx.enter_context(tc.tile_pool(name="consts", bufs=1))
+        hid = ctx.enter_context(tc.tile_pool(name="hid", bufs=HID_CHUNKS))
+        raw = ctx.enter_context(tc.tile_pool(name="raw", bufs=4))
+        work = ctx.enter_context(tc.tile_pool(name="work", bufs=3))
+        mx = ctx.enter_context(tc.tile_pool(name="mx", bufs=3))
+        results = ctx.enter_context(tc.tile_pool(name="results", bufs=M_TILES))
+        psum = ctx.enter_context(tc.psum_pool(name="psum", bufs=1))
+
+
+        vec_rows = consts.tile([P, P], BF16)
+        nc.vector.memset(vec_rows[:], 0.0)
+        nc.scalar.dma_start(
+            out=vec_rows[0:M_TILES, :], in_=connection_history.rearrange("(m j) -> m j", j=P)
+        )
+        nc.scalar.dma_start(
+            out=vec_rows[M_TILES : 2 * M_TILES, :],
+            in_=connection_strength.rearrange("(m j) -> m j", j=P),
+        )
+        decay_bf16 = consts.tile([P, 1], BF16)
+        nc.scalar.dma_start(out=decay_bf16[:], in_=connection_decay.partition_broadcast(P))
+        decay = consts.tile([P, 1], F32)
+        nc.vector.tensor_copy(out=decay[:], in_=decay_bf16[:])
+
+        identity = consts.tile([P, P], BF16)
+        make_identity(nc, identity[:])
+        vec_psum = psum.tile([P, P], BF16, name="vec_psum", tag="acc00")
+        nc.tensor.transpose(vec_psum[:], vec_rows[:], identity[:])
+        vec_cols = consts.tile([P, 2 * M_TILES], F32)
+        nc.vector.tensor_copy(out=vec_cols[:], in_=vec_psum[:, 0 : 2 * M_TILES])
+
+        pick = consts.tile([P, M_TILES, M_TILES], BF16)
+        nc.vector.memset(pick[:], 0.0)
+        for m in range(M_TILES):
+            nc.vector.memset(pick[:, m, m : m + 1], 1.0 / B)
+
+        hidden_rows = hidden.rearrange("(p r) j -> p r j", p=P)
+        half = HID_ROWS // 2
+        activity = psum.tile([P, M_TILES], F32, name="activity", tag="acc01")
+        for h in range(HID_CHUNKS):
+            hid_raw = hid.tile([P, HID_ROWS, H], BF16)
+            nc.sync.dma_start(out=hid_raw[:], in_=hidden_rows[:, h * HID_ROWS : (h + 1) * HID_ROWS, :])
+            hid_abs = hid.tile([P, HID_ROWS, H], BF16)
+            nc.scalar.activation(out=hid_abs[:, 0:half, :], in_=hid_raw[:, 0:half, :], func=ACT.Abs)
+            nc.vector.scalar_tensor_tensor(
+                out=hid_abs[:, half:HID_ROWS, :],
+                in0=hid_raw[:, half:HID_ROWS, :],
+                scalar=-1.0,
+                in1=hid_raw[:, half:HID_ROWS, :],
+                op0=ALU.mult,
+                op1=ALU.max,
+            )
+            for r in range(HID_ROWS):
+                for m in range(M_TILES):
+                    nc.tensor.matmul(
+                        out=activity[:],
+                        lhsT=hid_abs[:, r, m * P : (m + 1) * P],
+                        rhs=pick[:, m, :],
+                        start=(h == 0 and r == 0 and m == 0),
+                        stop=(h == HID_CHUNKS - 1 and r == HID_ROWS - 1 and m == M_TILES - 1),
+                    )
+
+        gate_in = consts.tile([P, M_TILES], F32)
+        nc.vector.scalar_tensor_tensor(
+            out=gate_in[:],
+            in0=vec_cols[:, 0:M_TILES],
+            scalar=decay[:, 0:1],
+            in1=activity[:],
+            op0=ALU.mult,
+            op1=ALU.add,
+        )
+        gate = consts.tile([P, M_TILES], F32)
+        nc.scalar.activation(out=gate[:], in_=gate_in[:], func=ACT.Sigmoid)
+        cs = consts.tile([P, M_TILES], F32)
+        nc.vector.tensor_mul(out=cs[:], in0=gate[:], in1=vec_cols[:, M_TILES : 2 * M_TILES])
+
+        g_passes = grad_out.rearrange("(c p t) j -> c p t j", p=P, t=PACK)
+        u_passes = update.rearrange("(c p t) j -> c p t j", p=P, t=PACK)
+        rh_passes = rh.rearrange("(c p t) j -> c p t j", p=P, t=PACK)
+        x_passes = x.rearrange("(c p t) j -> c p t j", p=P, t=PACK)
+
+        windows = (slice(0, N_PASS), slice(C - N_PASS, C))
+        acc = [
+            [psum.tile([P, N_PASS], F32, name="acc%d%d" % (m, n), tag="acc%d%d" % (m, n)) for n in range(2)]
+            for m in range(M_TILES)
+        ]
+
+        for c in range(PASSES):
+            g_raw = raw.tile([P, PACK, H], BF16)
+            nc.sync.dma_start(out=g_raw[:], in_=g_passes[c])
+            u_raw = raw.tile([P, PACK, H], BF16)
+            nc.sync.dma_start(out=u_raw[:], in_=u_passes[c])
+            rh_raw = raw.tile([P, PACK, H], BF16)
+            nc.sync.dma_start(out=rh_raw[:], in_=rh_passes[c])
+            x_raw = raw.tile([P, PACK, I], BF16)
+            nc.sync.dma_start(out=x_raw[:], in_=x_passes[c])
+
+            gu_rows = work.tile([P, PACK, H], BF16)
+            nc.vector.tensor_mul(out=gu_rows[:], in0=g_raw[:], in1=u_raw[:])
+            gu_grouped = work.tile([P, H, PACK], BF16, align_bytes=64)
+            regroup(nc.vector.tensor_copy, gu_grouped[:], gu_rows[:])
+            xr_grouped = work.tile([P, C, PACK], BF16, align_bytes=64)
+            regroup(nc.scalar.copy, xr_grouped[:, I:C, :], rh_raw[:])
+            regroup(nc.scalar.copy, xr_grouped[:, 0:I, :], x_raw[:])
+
+            gu_codes = mx.tile([P, H], U32, align_bytes=64)
+            gu_scales = mx.tile([P, H], U8, align_bytes=64)
+            xr_codes = mx.tile([P, C], U32, align_bytes=64)
+            xr_scales = mx.tile([P, C], U8, align_bytes=64)
+            nc.vector.quantize_mx(
+                out=xr_codes[:, I:C].bitcast(E4M3_X4),
+                scales=xr_scales[:, I:C],
+                in_=xr_grouped[:, I:C, :].rearrange("p w t -> p (w t)"),
+            )
+            nc.vector.quantize_mx(
+                out=gu_codes[:].bitcast(E5M2_X4),
+                scales=gu_scales[:],
+                in_=gu_grouped[:].rearrange("p w t -> p (w t)"),
+            )
+            nc.vector.quantize_mx(
+                out=xr_codes[:, 0:I].bitcast(E4M3_X4),
+                scales=xr_scales[:, 0:I],
+                in_=xr_grouped[:, 0:I, :].rearrange("p w t -> p (w t)"),
+            )
+
+            for m in range(M_TILES):
+                for n in range(2):
+                    nc.tensor.matmul_mx(
+                        out=acc[m][n][:],
+                        lhsT=gu_codes[:, m * P : (m + 1) * P].bitcast(E5M2_X4),
+                        lhsT_scale=gu_scales[:, m * P : (m + 1) * P],
+                        rhs=xr_codes[:, windows[n]].bitcast(E4M3_X4),
+                        rhs_scale=xr_scales[:, windows[n]],
+                        start=(c == 0),
+                        stop=(c == PASSES - 1),
+                    )
+
+        kept = C // 2
+        for m in range(M_TILES):
+            result = results.tile([P, C], F32)
+            nc.vector.tensor_scalar_mul(
+                out=result[:, 0:kept], in0=acc[m][0][:, 0:kept], scalar1=cs[:, m : m + 1]
+            )
+            nc.scalar.activation(
+                out=result[:, kept:C],
+                in_=acc[m][1][:, N_PASS - kept : N_PASS],
+                func=ACT.Copy,
+                scale=cs[:, m : m + 1],
+            )
+            nc.sync.dma_start(out=out[m * P : (m + 1) * P, :], in_=result[:])

@@ -7,6 +7,7 @@ F32 = mybir.dt.float32
 BF16 = mybir.dt.bfloat16
 U32 = mybir.dt.uint32
 U8 = mybir.dt.uint8
+I32 = mybir.dt.int32
 E4M3_X4 = mybir.dt.float8_e4m3fn_x4
 E5M2_X4 = mybir.dt.float8_e5m2_x4
 ALU = mybir.AluOpType
@@ -22,6 +23,7 @@ M_TILES = H // P
 N_PASS = 512
 HID_CHUNKS = 4
 HID_ROWS = B // P // HID_CHUNKS
+NO_SIGNS = 0x7FFF7FFF
 
 FLOPS = 2 * B * H * C
 BYTES = 2 * (B * I + 4 * B * H + 2 * H + 1) + 4 * H * C
@@ -50,14 +52,19 @@ def tile_persistentgrucell_pb_t_kernel(
 ):
     nc = tc.nc
     with ExitStack() as ctx:
+        ctx.enter_context(tc.manual_schedule())
         consts = ctx.enter_context(tc.tile_pool(name="consts", bufs=1))
         hid = ctx.enter_context(tc.tile_pool(name="hid", bufs=HID_CHUNKS))
-        raw = ctx.enter_context(tc.tile_pool(name="raw", bufs=4))
+        raw = ctx.enter_context(tc.tile_pool(name="raw", bufs=5))
         work = ctx.enter_context(tc.tile_pool(name="work", bufs=3))
         mx = ctx.enter_context(tc.tile_pool(name="mx", bufs=3))
         results = ctx.enter_context(tc.tile_pool(name="results", bufs=M_TILES))
         psum = ctx.enter_context(tc.psum_pool(name="psum", bufs=1))
 
+
+        warm = consts.tile([P, 1], F32)
+        nc.vector.memset(warm[:], 0.0)
+        nc.scalar.activation(out=warm[:], in_=warm[:], func=ACT.Sigmoid)
 
         vec_rows = consts.tile([P, P], BF16)
         nc.vector.memset(vec_rows[:], 0.0)
@@ -70,15 +77,8 @@ def tile_persistentgrucell_pb_t_kernel(
         )
         decay_bf16 = consts.tile([P, 1], BF16)
         nc.scalar.dma_start(out=decay_bf16[:], in_=connection_decay.partition_broadcast(P))
-        decay = consts.tile([P, 1], F32)
-        nc.vector.tensor_copy(out=decay[:], in_=decay_bf16[:])
-
         identity = consts.tile([P, P], BF16)
         make_identity(nc, identity[:])
-        vec_psum = psum.tile([P, P], BF16, name="vec_psum", tag="acc00")
-        nc.tensor.transpose(vec_psum[:], vec_rows[:], identity[:])
-        vec_cols = consts.tile([P, 2 * M_TILES], F32)
-        nc.vector.tensor_copy(out=vec_cols[:], in_=vec_psum[:, 0 : 2 * M_TILES])
 
         pick = consts.tile([P, M_TILES, M_TILES], BF16)
         nc.vector.memset(pick[:], 0.0)
@@ -86,20 +86,17 @@ def tile_persistentgrucell_pb_t_kernel(
             nc.vector.memset(pick[:, m, m : m + 1], 1.0 / B)
 
         hidden_rows = hidden.rearrange("(p r) j -> p r j", p=P)
-        half = HID_ROWS // 2
         activity = psum.tile([P, M_TILES], F32, name="activity", tag="acc01")
         for h in range(HID_CHUNKS):
             hid_raw = hid.tile([P, HID_ROWS, H], BF16)
             nc.sync.dma_start(out=hid_raw[:], in_=hidden_rows[:, h * HID_ROWS : (h + 1) * HID_ROWS, :])
             hid_abs = hid.tile([P, HID_ROWS, H], BF16)
-            nc.scalar.activation(out=hid_abs[:, 0:half, :], in_=hid_raw[:, 0:half, :], func=ACT.Abs)
-            nc.vector.scalar_tensor_tensor(
-                out=hid_abs[:, half:HID_ROWS, :],
-                in0=hid_raw[:, half:HID_ROWS, :],
-                scalar=-1.0,
-                in1=hid_raw[:, half:HID_ROWS, :],
-                op0=ALU.mult,
-                op1=ALU.max,
+            nc.vector.tensor_scalar(
+                out=hid_abs[:].rearrange("p r j -> p (r j)").bitcast(I32),
+                in0=hid_raw[:].rearrange("p r j -> p (r j)").bitcast(I32),
+                scalar1=NO_SIGNS,
+                scalar2=None,
+                op0=ALU.bitwise_and,
             )
             for r in range(HID_ROWS):
                 for m in range(M_TILES):
@@ -111,6 +108,12 @@ def tile_persistentgrucell_pb_t_kernel(
                         stop=(h == HID_CHUNKS - 1 and r == HID_ROWS - 1 and m == M_TILES - 1),
                     )
 
+        vec_psum = psum.tile([P, P], BF16, name="vec_psum", tag="acc00")
+        nc.tensor.transpose(vec_psum[:], vec_rows[:], identity[:])
+        vec_cols = consts.tile([P, 2 * M_TILES], F32)
+        nc.vector.tensor_copy(out=vec_cols[:], in_=vec_psum[:, 0 : 2 * M_TILES])
+        decay = consts.tile([P, 1], F32)
+        nc.vector.tensor_copy(out=decay[:], in_=decay_bf16[:])
         gate_in = consts.tile([P, M_TILES], F32)
         nc.vector.scalar_tensor_tensor(
             out=gate_in[:],
@@ -120,10 +123,12 @@ def tile_persistentgrucell_pb_t_kernel(
             op0=ALU.mult,
             op1=ALU.add,
         )
-        gate = consts.tile([P, M_TILES], F32)
-        nc.scalar.activation(out=gate[:], in_=gate_in[:], func=ACT.Sigmoid)
         cs = consts.tile([P, M_TILES], F32)
-        nc.vector.tensor_mul(out=cs[:], in0=gate[:], in1=vec_cols[:, M_TILES : 2 * M_TILES])
+
+        def finish_cs():
+            gate = consts.tile([P, M_TILES], F32)
+            nc.scalar.activation(out=gate[:], in_=gate_in[:], func=ACT.Sigmoid)
+            nc.vector.tensor_mul(out=cs[:], in0=gate[:], in1=vec_cols[:, M_TILES : 2 * M_TILES])
 
         g_passes = grad_out.rearrange("(c p t) j -> c p t j", p=P, t=PACK)
         u_passes = update.rearrange("(c p t) j -> c p t j", p=P, t=PACK)
@@ -136,55 +141,73 @@ def tile_persistentgrucell_pb_t_kernel(
             for m in range(M_TILES)
         ]
 
-        for c in range(PASSES):
-            g_raw = raw.tile([P, PACK, H], BF16)
-            nc.sync.dma_start(out=g_raw[:], in_=g_passes[c])
-            u_raw = raw.tile([P, PACK, H], BF16)
-            nc.sync.dma_start(out=u_raw[:], in_=u_passes[c])
-            rh_raw = raw.tile([P, PACK, H], BF16)
+        def one_pass(c, pieces):
+            rh_raw = raw.tile([P, PACK, H], BF16, name="rh_raw")
             nc.sync.dma_start(out=rh_raw[:], in_=rh_passes[c])
-            x_raw = raw.tile([P, PACK, I], BF16)
+            x_raw = raw.tile([P, PACK, I], BF16, name="x_raw")
             nc.sync.dma_start(out=x_raw[:], in_=x_passes[c])
+            g_raw = raw.tile([P, PACK, H], BF16, name="g_raw")
+            nc.sync.dma_start(out=g_raw[:], in_=g_passes[c])
+            u_raw = raw.tile([P, PACK, H], BF16, name="u_raw")
+            nc.sync.dma_start(out=u_raw[:], in_=u_passes[c])
 
-            gu_rows = work.tile([P, PACK, H], BF16)
-            nc.vector.tensor_mul(out=gu_rows[:], in0=g_raw[:], in1=u_raw[:])
-            gu_grouped = work.tile([P, H, PACK], BF16, align_bytes=64)
-            regroup(nc.vector.tensor_copy, gu_grouped[:], gu_rows[:])
-            xr_grouped = work.tile([P, C, PACK], BF16, align_bytes=64)
+            xr_grouped = work.tile([P, C, PACK], BF16, name="xr_grouped", align_bytes=64)
             regroup(nc.scalar.copy, xr_grouped[:, I:C, :], rh_raw[:])
             regroup(nc.scalar.copy, xr_grouped[:, 0:I, :], x_raw[:])
 
-            gu_codes = mx.tile([P, H], U32, align_bytes=64)
-            gu_scales = mx.tile([P, H], U8, align_bytes=64)
-            xr_codes = mx.tile([P, C], U32, align_bytes=64)
-            xr_scales = mx.tile([P, C], U8, align_bytes=64)
-            nc.vector.quantize_mx(
-                out=xr_codes[:, I:C].bitcast(E4M3_X4),
-                scales=xr_scales[:, I:C],
-                in_=xr_grouped[:, I:C, :].rearrange("p w t -> p (w t)"),
-            )
-            nc.vector.quantize_mx(
-                out=gu_codes[:].bitcast(E5M2_X4),
-                scales=gu_scales[:],
-                in_=gu_grouped[:].rearrange("p w t -> p (w t)"),
-            )
-            nc.vector.quantize_mx(
-                out=xr_codes[:, 0:I].bitcast(E4M3_X4),
-                scales=xr_scales[:, 0:I],
-                in_=xr_grouped[:, 0:I, :].rearrange("p w t -> p (w t)"),
-            )
+            gu_codes = mx.tile([P, H], U32, name="gu_codes", align_bytes=64)
+            gu_scales = mx.tile([P, H], U8, name="gu_scales", align_bytes=64)
+            xr_codes = mx.tile([P, C], U32, name="xr_codes", align_bytes=64)
+            xr_scales = mx.tile([P, C], U8, name="xr_scales", align_bytes=64)
 
-            for m in range(M_TILES):
-                for n in range(2):
-                    nc.tensor.matmul_mx(
-                        out=acc[m][n][:],
-                        lhsT=gu_codes[:, m * P : (m + 1) * P].bitcast(E5M2_X4),
-                        lhsT_scale=gu_scales[:, m * P : (m + 1) * P],
-                        rhs=xr_codes[:, windows[n]].bitcast(E4M3_X4),
-                        rhs_scale=xr_scales[:, windows[n]],
-                        start=(c == 0),
-                        stop=(c == PASSES - 1),
+            gu_rows = work.tile([P, PACK, H], BF16, name="gu_rows")
+            gu_grouped = work.tile([P, H, PACK], BF16, name="gu_grouped", align_bytes=64)
+            width = H // pieces
+
+            def finish(k):
+                cols = slice(k * width, (k + 1) * width)
+                nc.vector.quantize_mx(
+                    out=gu_codes[:, cols].bitcast(E5M2_X4),
+                    scales=gu_scales[:, cols],
+                    in_=gu_grouped[:, cols, :].rearrange("p w t -> p (w t)"),
+                )
+                for m in range(k * width // P, (k + 1) * width // P):
+                    for n in range(2):
+                        nc.tensor.matmul_mx(
+                            out=acc[m][n][:],
+                            lhsT=gu_codes[:, m * P : (m + 1) * P].bitcast(E5M2_X4),
+                            lhsT_scale=gu_scales[:, m * P : (m + 1) * P],
+                            rhs=xr_codes[:, windows[n]].bitcast(E4M3_X4),
+                            rhs_scale=xr_scales[:, windows[n]],
+                            start=(c == 0),
+                            stop=(c == PASSES - 1),
+                        )
+
+            for k in range(pieces):
+                cols = slice(k * width, (k + 1) * width)
+                nc.vector.tensor_mul(out=gu_rows[:, :, cols], in0=g_raw[:, :, cols], in1=u_raw[:, :, cols])
+                if k == 0:
+                    nc.vector.quantize_mx(
+                        out=xr_codes[:, I:C].bitcast(E4M3_X4),
+                        scales=xr_scales[:, I:C],
+                        in_=xr_grouped[:, I:C, :].rearrange("p w t -> p (w t)"),
                     )
+                else:
+                    finish(k - 1)
+                regroup(nc.vector.tensor_copy, gu_grouped[:, cols, :], gu_rows[:, :, cols])
+                if k == 0:
+                    nc.vector.quantize_mx(
+                        out=xr_codes[:, 0:I].bitcast(E4M3_X4),
+                        scales=xr_scales[:, 0:I],
+                        in_=xr_grouped[:, 0:I, :].rearrange("p w t -> p (w t)"),
+                    )
+            finish(pieces - 1)
+
+        one_pass(0, 1)
+        finish_cs()
+        for c in range(1, PASSES - 1):
+            one_pass(c, 1)
+        one_pass(PASSES - 1, M_TILES)
 
         kept = C // 2
         for m in range(M_TILES):
@@ -198,4 +221,5 @@ def tile_persistentgrucell_pb_t_kernel(
                 func=ACT.Copy,
                 scale=cs[:, m : m + 1],
             )
-            nc.sync.dma_start(out=out[m * P : (m + 1) * P, :], in_=result[:])
+            nc.scalar.dma_start(out=out[m * P : (m + 1) * P, kept:C], in_=result[:, kept:C])
+            nc.sync.dma_start(out=out[m * P : (m + 1) * P, 0:kept], in_=result[:, 0:kept])

@@ -75,18 +75,19 @@ def tile_persistentgrucell_pb_t_kernel(
             out=vec_rows[M_TILES : 2 * M_TILES, :],
             in_=connection_strength.rearrange("(m j) -> m j", j=P),
         )
-        decay_bf16 = consts.tile([P, 1], BF16)
-        nc.scalar.dma_start(out=decay_bf16[:], in_=connection_decay.partition_broadcast(P))
         identity = consts.tile([P, P], BF16)
         make_identity(nc, identity[:])
 
-        pick = consts.tile([P, M_TILES, M_TILES], BF16)
+        decay_bf16 = consts.tile([M_TILES, 1], BF16)
+        nc.scalar.dma_start(out=decay_bf16[:], in_=connection_decay.partition_broadcast(M_TILES))
+
+        pick = consts.tile([P, M_TILES, 2 * M_TILES], BF16)
         nc.vector.memset(pick[:], 0.0)
         for m in range(M_TILES):
             nc.vector.memset(pick[:, m, m : m + 1], 1.0 / B)
 
         hidden_rows = hidden.rearrange("(p r) j -> p r j", p=P)
-        activity = psum.tile([P, M_TILES], F32, name="activity", tag="acc01")
+        gate_psum = psum.tile([P, 2 * M_TILES], F32, name="gate_psum", tag="acc00")
         for h in range(HID_CHUNKS):
             hid_raw = hid.tile([P, HID_ROWS, H], BF16)
             nc.sync.dma_start(out=hid_raw[:], in_=hidden_rows[:, h * HID_ROWS : (h + 1) * HID_ROWS, :])
@@ -101,34 +102,29 @@ def tile_persistentgrucell_pb_t_kernel(
             for r in range(HID_ROWS):
                 for m in range(M_TILES):
                     nc.tensor.matmul(
-                        out=activity[:],
+                        out=gate_psum[:],
                         lhsT=hid_abs[:, r, m * P : (m + 1) * P],
                         rhs=pick[:, m, :],
                         start=(h == 0 and r == 0 and m == 0),
-                        stop=(h == HID_CHUNKS - 1 and r == HID_ROWS - 1 and m == M_TILES - 1),
+                        stop=False,
                     )
 
-        vec_psum = psum.tile([P, P], BF16, name="vec_psum", tag="acc00")
-        nc.tensor.transpose(vec_psum[:], vec_rows[:], identity[:])
-        vec_cols = consts.tile([P, 2 * M_TILES], F32)
-        nc.vector.tensor_copy(out=vec_cols[:], in_=vec_psum[:, 0 : 2 * M_TILES])
-        decay = consts.tile([P, 1], F32)
+        decay = consts.tile([M_TILES, 1], F32)
         nc.vector.tensor_copy(out=decay[:], in_=decay_bf16[:])
-        gate_in = consts.tile([P, M_TILES], F32)
-        nc.vector.scalar_tensor_tensor(
-            out=gate_in[:],
-            in0=vec_cols[:, 0:M_TILES],
-            scalar=decay[:, 0:1],
-            in1=activity[:],
-            op0=ALU.mult,
-            op1=ALU.add,
+        spread = consts.tile([P, 2 * M_TILES], BF16)
+        nc.vector.tensor_copy(out=spread[:], in_=identity[:, 0 : 2 * M_TILES])
+        nc.vector.tensor_scalar_mul(
+            out=spread[0:M_TILES, 0:M_TILES], in0=identity[0:M_TILES, 0:M_TILES], scalar1=decay[:, 0:1]
         )
+        nc.tensor.matmul(out=gate_psum[:], lhsT=vec_rows[:], rhs=spread[:], start=False, stop=True)
+        gate_in = consts.tile([P, 2 * M_TILES], F32)
+        nc.vector.tensor_copy(out=gate_in[:], in_=gate_psum[:])
         cs = consts.tile([P, M_TILES], F32)
 
         def finish_cs():
             gate = consts.tile([P, M_TILES], F32)
-            nc.scalar.activation(out=gate[:], in_=gate_in[:], func=ACT.Sigmoid)
-            nc.vector.tensor_mul(out=cs[:], in0=gate[:], in1=vec_cols[:, M_TILES : 2 * M_TILES])
+            nc.scalar.activation(out=gate[:], in_=gate_in[:, 0:M_TILES], func=ACT.Sigmoid)
+            nc.vector.tensor_mul(out=cs[:], in0=gate[:], in1=gate_in[:, M_TILES : 2 * M_TILES])
 
         g_passes = grad_out.rearrange("(c p t) j -> c p t j", p=P, t=PACK)
         u_passes = update.rearrange("(c p t) j -> c p t j", p=P, t=PACK)
@@ -212,14 +208,18 @@ def tile_persistentgrucell_pb_t_kernel(
         kept = C // 2
         for m in range(M_TILES):
             result = results.tile([P, C], F32)
-            nc.vector.tensor_scalar_mul(
-                out=result[:, 0:kept], in0=acc[m][0][:, 0:kept], scalar1=cs[:, m : m + 1]
-            )
             nc.scalar.activation(
                 out=result[:, kept:C],
                 in_=acc[m][1][:, N_PASS - kept : N_PASS],
                 func=ACT.Copy,
                 scale=cs[:, m : m + 1],
             )
-            nc.scalar.dma_start(out=out[m * P : (m + 1) * P, kept:C], in_=result[:, kept:C])
-            nc.sync.dma_start(out=out[m * P : (m + 1) * P, 0:kept], in_=result[:, 0:kept])
+            if m < M_TILES // 2:
+                nc.scalar.activation(
+                    out=result[:, 0:kept], in_=acc[m][0][:, 0:kept], func=ACT.Copy, scale=cs[:, m : m + 1]
+                )
+            else:
+                nc.vector.tensor_scalar_mul(
+                    out=result[:, 0:kept], in0=acc[m][0][:, 0:kept], scalar1=cs[:, m : m + 1]
+                )
+            nc.sync.dma_start(out=out[m * P : (m + 1) * P, :], in_=result[:])

@@ -21,8 +21,9 @@ K_PASS = P * PACK
 PASSES = B // K_PASS
 M_TILES = H // P
 N_PASS = 512
-HID_CHUNKS = 4
+HID_CHUNKS = 8
 HID_ROWS = B // P // HID_CHUNKS
+HID_PLAN = ((0,), (1,), (2,), (3,), (4, 5), (6, 7), (), ())
 NO_SIGNS = 0x7FFF7FFF
 
 FLOPS = 2 * B * H * C
@@ -54,13 +55,12 @@ def tile_persistentgrucell_pb_t_kernel(
     with ExitStack() as ctx:
         ctx.enter_context(tc.manual_schedule())
         consts = ctx.enter_context(tc.tile_pool(name="consts", bufs=1))
-        hid = ctx.enter_context(tc.tile_pool(name="hid", bufs=HID_CHUNKS))
+        hid = ctx.enter_context(tc.tile_pool(name="hid", bufs=4))
         raw = ctx.enter_context(tc.tile_pool(name="raw", bufs=5))
         work = ctx.enter_context(tc.tile_pool(name="work", bufs=3))
-        mx = ctx.enter_context(tc.tile_pool(name="mx", bufs=3))
+        mx = ctx.enter_context(tc.tile_pool(name="mx", bufs=PASSES))
         results = ctx.enter_context(tc.tile_pool(name="results", bufs=M_TILES))
         psum = ctx.enter_context(tc.psum_pool(name="psum", bufs=1))
-
 
         warm = consts.tile([P, 1], F32)
         nc.vector.memset(warm[:], 0.0)
@@ -87,11 +87,19 @@ def tile_persistentgrucell_pb_t_kernel(
             nc.vector.memset(pick[:, m, m : m + 1], 1.0 / B)
 
         hidden_rows = hidden.rearrange("(p r) j -> p r j", p=P)
-        gate_psum = psum.tile([P, 2 * M_TILES], F32, name="gate_psum", tag="acc00")
-        for h in range(HID_CHUNKS):
-            hid_raw = hid.tile([P, HID_ROWS, H], BF16)
+        LAST = (M_TILES - 1, 1)
+        gate_psum = psum.tile([P, 2 * M_TILES], F32, name="gate_psum", tag="acc%d%d" % LAST)
+        spread = consts.tile([P, 2 * M_TILES], BF16)
+        gate_in = consts.tile([P, 2 * M_TILES], F32)
+        cs = consts.tile([P, M_TILES], F32)
+
+        def load_hidden(h):
+            hid_raw = hid.tile([P, HID_ROWS, H], BF16, name="hid_raw")
             nc.sync.dma_start(out=hid_raw[:], in_=hidden_rows[:, h * HID_ROWS : (h + 1) * HID_ROWS, :])
-            hid_abs = hid.tile([P, HID_ROWS, H], BF16)
+            return hid_raw
+
+        def sum_hidden(h, hid_raw):
+            hid_abs = hid.tile([P, HID_ROWS, H], BF16, name="hid_abs")
             nc.vector.tensor_scalar(
                 out=hid_abs[:].rearrange("p r j -> p (r j)").bitcast(I32),
                 in0=hid_raw[:].rearrange("p r j -> p (r j)").bitcast(I32),
@@ -109,22 +117,16 @@ def tile_persistentgrucell_pb_t_kernel(
                         stop=False,
                     )
 
-        decay = consts.tile([M_TILES, 1], F32)
-        nc.vector.tensor_copy(out=decay[:], in_=decay_bf16[:])
-        spread = consts.tile([P, 2 * M_TILES], BF16)
-        nc.vector.tensor_copy(out=spread[:], in_=identity[:, 0 : 2 * M_TILES])
-        nc.vector.tensor_scalar_mul(
-            out=spread[0:M_TILES, 0:M_TILES], in0=identity[0:M_TILES, 0:M_TILES], scalar1=decay[:, 0:1]
-        )
-        nc.tensor.matmul(out=gate_psum[:], lhsT=vec_rows[:], rhs=spread[:], start=False, stop=True)
-        gate_in = consts.tile([P, 2 * M_TILES], F32)
-        nc.vector.tensor_copy(out=gate_in[:], in_=gate_psum[:])
-        cs = consts.tile([P, M_TILES], F32)
+        def make_spread():
+            decay = consts.tile([M_TILES, 1], F32)
+            nc.vector.tensor_copy(out=decay[:], in_=decay_bf16[:])
+            nc.vector.tensor_copy(out=spread[:], in_=identity[:, 0 : 2 * M_TILES])
+            nc.vector.tensor_scalar_mul(
+                out=spread[0:M_TILES, 0:M_TILES], in0=identity[0:M_TILES, 0:M_TILES], scalar1=decay[:, 0:1]
+            )
 
-        def finish_cs():
-            gate = consts.tile([P, M_TILES], F32)
-            nc.scalar.activation(out=gate[:], in_=gate_in[:, 0:M_TILES], func=ACT.Sigmoid)
-            nc.vector.tensor_mul(out=cs[:], in0=gate[:], in1=gate_in[:, M_TILES : 2 * M_TILES])
+        gate = consts.tile([P, M_TILES], F32)
+        GATE_PASS = max([c for c in range(PASSES) if HID_PLAN[c]])
 
         g_passes = grad_out.rearrange("(c p t) j -> c p t j", p=P, t=PACK)
         u_passes = update.rearrange("(c p t) j -> c p t j", p=P, t=PACK)
@@ -132,76 +134,127 @@ def tile_persistentgrucell_pb_t_kernel(
         x_passes = x.rearrange("(c p t) j -> c p t j", p=P, t=PACK)
 
         windows = (slice(0, N_PASS), slice(C - N_PASS, C))
-        acc = [
-            [psum.tile([P, N_PASS], F32, name="acc%d%d" % (m, n), tag="acc%d%d" % (m, n)) for n in range(2)]
-            for m in range(M_TILES)
-        ]
+        acc = {}
+        for m in range(M_TILES):
+            for n in range(2):
+                if (m, n) != LAST:
+                    acc[(m, n)] = psum.tile([P, N_PASS], F32, name="acc%d%d" % (m, n), tag="acc%d%d" % (m, n))
+        codes = {}
+        late = []
+
+        def multiply(c, m, n):
+            gu_codes, gu_scales, xr_codes, xr_scales = codes[c]
+            nc.tensor.matmul_mx(
+                out=acc[(m, n)][:],
+                lhsT=gu_codes[:, m * P : (m + 1) * P].bitcast(E5M2_X4),
+                lhsT_scale=gu_scales[:, m * P : (m + 1) * P],
+                rhs=xr_codes[:, windows[n]].bitcast(E4M3_X4),
+                rhs_scale=xr_scales[:, windows[n]],
+                start=(c == 0),
+                stop=(c == PASSES - 1),
+            )
 
         def one_pass(c, pieces):
             rh_raw = raw.tile([P, PACK, H], BF16, name="rh_raw")
-            nc.sync.dma_start(out=rh_raw[:], in_=rh_passes[c])
             x_raw = raw.tile([P, PACK, I], BF16, name="x_raw")
-            nc.sync.dma_start(out=x_raw[:], in_=x_passes[c])
             g_raw = raw.tile([P, PACK, H], BF16, name="g_raw")
-            nc.sync.dma_start(out=g_raw[:], in_=g_passes[c])
             u_raw = raw.tile([P, PACK, H], BF16, name="u_raw")
-            nc.sync.dma_start(out=u_raw[:], in_=u_passes[c])
+            if c == 0:
+                nc.sync.dma_start(out=g_raw[:], in_=g_passes[c])
+                nc.sync.dma_start(out=u_raw[:], in_=u_passes[c])
+                nc.sync.dma_start(out=rh_raw[:], in_=rh_passes[c])
+                nc.sync.dma_start(out=x_raw[:], in_=x_passes[c])
+            else:
+                nc.sync.dma_start(out=rh_raw[:], in_=rh_passes[c])
+                nc.sync.dma_start(out=x_raw[:], in_=x_passes[c])
+                nc.sync.dma_start(out=g_raw[:], in_=g_passes[c])
+                nc.sync.dma_start(out=u_raw[:], in_=u_passes[c])
+            hid_raws = [(h, load_hidden(h)) for h in HID_PLAN[c]]
 
             xr_grouped = work.tile([P, C, PACK], BF16, name="xr_grouped", align_bytes=64)
             regroup(nc.scalar.copy, xr_grouped[:, I:C, :], rh_raw[:])
             regroup(nc.scalar.copy, xr_grouped[:, 0:I, :], x_raw[:])
+            if c == PASSES - 1:
+                nc.scalar.activation(out=gate[:], in_=gate_in[:, 0:M_TILES], func=ACT.Sigmoid)
 
             gu_codes = mx.tile([P, H], U32, name="gu_codes", align_bytes=64)
             gu_scales = mx.tile([P, H], U8, name="gu_scales", align_bytes=64)
             xr_codes = mx.tile([P, C], U32, name="xr_codes", align_bytes=64)
             xr_scales = mx.tile([P, C], U8, name="xr_scales", align_bytes=64)
+            codes[c] = (gu_codes, gu_scales, xr_codes, xr_scales)
 
             gu_rows = work.tile([P, PACK, H], BF16, name="gu_rows")
             gu_grouped = work.tile([P, H, PACK], BF16, name="gu_grouped", align_bytes=64)
             width = H // pieces
 
-            def finish(k):
+            def quantise_rh():
+                nc.vector.quantize_mx(
+                    out=xr_codes[:, I:C].bitcast(E4M3_X4),
+                    scales=xr_scales[:, I:C],
+                    in_=xr_grouped[:, I:C, :].rearrange("p w t -> p (w t)"),
+                )
+
+            def quantise_x():
+                nc.vector.quantize_mx(
+                    out=xr_codes[:, 0:I].bitcast(E4M3_X4),
+                    scales=xr_scales[:, 0:I],
+                    in_=xr_grouped[:, 0:I, :].rearrange("p w t -> p (w t)"),
+                )
+
+            def quantise_gu(k):
                 cols = slice(k * width, (k + 1) * width)
                 nc.vector.quantize_mx(
                     out=gu_codes[:, cols].bitcast(E5M2_X4),
                     scales=gu_scales[:, cols],
                     in_=gu_grouped[:, cols, :].rearrange("p w t -> p (w t)"),
                 )
+
+            def products(k):
                 for m in range(k * width // P, (k + 1) * width // P):
                     for n in range(2):
-                        nc.tensor.matmul_mx(
-                            out=acc[m][n][:],
-                            lhsT=gu_codes[:, m * P : (m + 1) * P].bitcast(E5M2_X4),
-                            lhsT_scale=gu_scales[:, m * P : (m + 1) * P],
-                            rhs=xr_codes[:, windows[n]].bitcast(E4M3_X4),
-                            rhs_scale=xr_scales[:, windows[n]],
-                            start=(c == 0),
-                            stop=(c == PASSES - 1),
-                        )
+                        if (m, n) in acc:
+                            multiply(c, m, n)
+                        else:
+                            late.append(c)
+
+            if c == 0:
+                nc.vector.tensor_mul(out=gu_rows[:], in0=g_raw[:], in1=u_raw[:])
+                make_spread()
+                regroup(nc.vector.tensor_copy, gu_grouped[:], gu_rows[:])
+                quantise_gu(0)
+                quantise_rh()
+                quantise_x()
+                for h, hid_raw in hid_raws:
+                    sum_hidden(h, hid_raw)
+                products(0)
+                return
 
             for k in range(pieces):
                 cols = slice(k * width, (k + 1) * width)
                 nc.vector.tensor_mul(out=gu_rows[:, :, cols], in0=g_raw[:, :, cols], in1=u_raw[:, :, cols])
                 if k == 0:
-                    nc.vector.quantize_mx(
-                        out=xr_codes[:, I:C].bitcast(E4M3_X4),
-                        scales=xr_scales[:, I:C],
-                        in_=xr_grouped[:, I:C, :].rearrange("p w t -> p (w t)"),
-                    )
+                    quantise_rh()
+                    if c == GATE_PASS + 1:
+                        nc.vector.tensor_copy(out=gate_in[:], in_=gate_psum[:])
+                        acc[LAST] = psum.tile([P, N_PASS], F32, name="acc%d%d" % LAST, tag="acc%d%d" % LAST)
+                        for cc in late:
+                            multiply(cc, LAST[0], LAST[1])
                 else:
-                    finish(k - 1)
+                    quantise_gu(k - 1)
+                    products(k - 1)
+                    if k == 1:
+                        nc.vector.tensor_mul(out=cs[:], in0=gate[:], in1=gate_in[:, M_TILES : 2 * M_TILES])
                 regroup(nc.vector.tensor_copy, gu_grouped[:, cols, :], gu_rows[:, :, cols])
                 if k == 0:
-                    nc.vector.quantize_mx(
-                        out=xr_codes[:, 0:I].bitcast(E4M3_X4),
-                        scales=xr_scales[:, 0:I],
-                        in_=xr_grouped[:, 0:I, :].rearrange("p w t -> p (w t)"),
-                    )
-            finish(pieces - 1)
+                    quantise_x()
+                    for h, hid_raw in hid_raws:
+                        sum_hidden(h, hid_raw)
+                    if c == GATE_PASS:
+                        nc.tensor.matmul(out=gate_psum[:], lhsT=vec_rows[:], rhs=spread[:], start=False, stop=True)
+            quantise_gu(pieces - 1)
+            products(pieces - 1)
 
-        one_pass(0, 1)
-        finish_cs()
-        for c in range(1, PASSES - 1):
+        for c in range(PASSES - 1):
             one_pass(c, 1)
         one_pass(PASSES - 1, M_TILES)
 
@@ -210,16 +263,16 @@ def tile_persistentgrucell_pb_t_kernel(
             result = results.tile([P, C], F32)
             nc.scalar.activation(
                 out=result[:, kept:C],
-                in_=acc[m][1][:, N_PASS - kept : N_PASS],
+                in_=acc[(m, 1)][:, N_PASS - kept : N_PASS],
                 func=ACT.Copy,
                 scale=cs[:, m : m + 1],
             )
             if m < M_TILES // 2:
                 nc.scalar.activation(
-                    out=result[:, 0:kept], in_=acc[m][0][:, 0:kept], func=ACT.Copy, scale=cs[:, m : m + 1]
+                    out=result[:, 0:kept], in_=acc[(m, 0)][:, 0:kept], func=ACT.Copy, scale=cs[:, m : m + 1]
                 )
             else:
                 nc.vector.tensor_scalar_mul(
-                    out=result[:, 0:kept], in0=acc[m][0][:, 0:kept], scalar1=cs[:, m : m + 1]
+                    out=result[:, 0:kept], in0=acc[(m, 0)][:, 0:kept], scalar1=cs[:, m : m + 1]
                 )
             nc.sync.dma_start(out=out[m * P : (m + 1) * P, :], in_=result[:])

@@ -23,7 +23,8 @@ M_TILES = H // P
 N_PASS = 512
 HID_CHUNKS = 8
 HID_ROWS = B // P // HID_CHUNKS
-HID_PLAN = ((0,), (1,), (2,), (3,), (4, 5), (6, 7), (), ())
+SCALAR_CHUNKS = (0, 1)
+SUM_ORDER = (0, 2, 3, 4, 1, 5, 6, 7)
 NO_SIGNS = 0x7FFF7FFF
 
 FLOPS = 2 * B * H * C
@@ -55,7 +56,9 @@ def tile_persistentgrucell_pb_t_kernel(
     with ExitStack() as ctx:
         ctx.enter_context(tc.manual_schedule())
         consts = ctx.enter_context(tc.tile_pool(name="consts", bufs=1))
-        hid = ctx.enter_context(tc.tile_pool(name="hid", bufs=4))
+        hid = ctx.enter_context(tc.tile_pool(name="hid", bufs=HID_CHUNKS))
+        hid2 = ctx.enter_context(tc.tile_pool(name="hid2", bufs=3))
+        hid3 = ctx.enter_context(tc.tile_pool(name="hid3", bufs=len(SCALAR_CHUNKS)))
         raw = ctx.enter_context(tc.tile_pool(name="raw", bufs=5))
         work = ctx.enter_context(tc.tile_pool(name="work", bufs=3))
         mx = ctx.enter_context(tc.tile_pool(name="mx", bufs=PASSES))
@@ -91,31 +94,8 @@ def tile_persistentgrucell_pb_t_kernel(
         gate_psum = psum.tile([P, 2 * M_TILES], F32, name="gate_psum", tag="acc%d%d" % LAST)
         spread = consts.tile([P, 2 * M_TILES], BF16)
         gate_in = consts.tile([P, 2 * M_TILES], F32)
+        gate = consts.tile([P, M_TILES], F32)
         cs = consts.tile([P, M_TILES], F32)
-
-        def load_hidden(h):
-            hid_raw = hid.tile([P, HID_ROWS, H], BF16, name="hid_raw")
-            nc.sync.dma_start(out=hid_raw[:], in_=hidden_rows[:, h * HID_ROWS : (h + 1) * HID_ROWS, :])
-            return hid_raw
-
-        def sum_hidden(h, hid_raw):
-            hid_abs = hid.tile([P, HID_ROWS, H], BF16, name="hid_abs")
-            nc.vector.tensor_scalar(
-                out=hid_abs[:].rearrange("p r j -> p (r j)").bitcast(I32),
-                in0=hid_raw[:].rearrange("p r j -> p (r j)").bitcast(I32),
-                scalar1=NO_SIGNS,
-                scalar2=None,
-                op0=ALU.bitwise_and,
-            )
-            for r in range(HID_ROWS):
-                for m in range(M_TILES):
-                    nc.tensor.matmul(
-                        out=gate_psum[:],
-                        lhsT=hid_abs[:, r, m * P : (m + 1) * P],
-                        rhs=pick[:, m, :],
-                        start=(h == 0 and r == 0 and m == 0),
-                        stop=False,
-                    )
 
         def make_spread():
             decay = consts.tile([M_TILES, 1], F32)
@@ -124,9 +104,7 @@ def tile_persistentgrucell_pb_t_kernel(
             nc.vector.tensor_scalar_mul(
                 out=spread[0:M_TILES, 0:M_TILES], in0=identity[0:M_TILES, 0:M_TILES], scalar1=decay[:, 0:1]
             )
-
-        gate = consts.tile([P, M_TILES], F32)
-        GATE_PASS = max([c for c in range(PASSES) if HID_PLAN[c]])
+            nc.tensor.matmul(out=gate_psum[:], lhsT=vec_rows[:], rhs=spread[:], start=True, stop=False)
 
         g_passes = grad_out.rearrange("(c p t) j -> c p t j", p=P, t=PACK)
         u_passes = update.rearrange("(c p t) j -> c p t j", p=P, t=PACK)
@@ -140,7 +118,6 @@ def tile_persistentgrucell_pb_t_kernel(
                 if (m, n) != LAST:
                     acc[(m, n)] = psum.tile([P, N_PASS], F32, name="acc%d%d" % (m, n), tag="acc%d%d" % (m, n))
         codes = {}
-        late = []
 
         def multiply(c, m, n):
             gu_codes, gu_scales, xr_codes, xr_scales = codes[c]
@@ -154,7 +131,7 @@ def tile_persistentgrucell_pb_t_kernel(
                 stop=(c == PASSES - 1),
             )
 
-        def one_pass(c, pieces):
+        def one_pass(c):
             rh_raw = raw.tile([P, PACK, H], BF16, name="rh_raw")
             x_raw = raw.tile([P, PACK, I], BF16, name="x_raw")
             g_raw = raw.tile([P, PACK, H], BF16, name="g_raw")
@@ -169,13 +146,10 @@ def tile_persistentgrucell_pb_t_kernel(
                 nc.sync.dma_start(out=x_raw[:], in_=x_passes[c])
                 nc.sync.dma_start(out=g_raw[:], in_=g_passes[c])
                 nc.sync.dma_start(out=u_raw[:], in_=u_passes[c])
-            hid_raws = [(h, load_hidden(h)) for h in HID_PLAN[c]]
 
             xr_grouped = work.tile([P, C, PACK], BF16, name="xr_grouped", align_bytes=64)
             regroup(nc.scalar.copy, xr_grouped[:, I:C, :], rh_raw[:])
             regroup(nc.scalar.copy, xr_grouped[:, 0:I, :], x_raw[:])
-            if c == PASSES - 1:
-                nc.scalar.activation(out=gate[:], in_=gate_in[:, 0:M_TILES], func=ACT.Sigmoid)
 
             gu_codes = mx.tile([P, H], U32, name="gu_codes", align_bytes=64)
             gu_scales = mx.tile([P, H], U8, name="gu_scales", align_bytes=64)
@@ -185,7 +159,6 @@ def tile_persistentgrucell_pb_t_kernel(
 
             gu_rows = work.tile([P, PACK, H], BF16, name="gu_rows")
             gu_grouped = work.tile([P, H, PACK], BF16, name="gu_grouped", align_bytes=64)
-            width = H // pieces
 
             def quantise_rh():
                 nc.vector.quantize_mx(
@@ -201,62 +174,67 @@ def tile_persistentgrucell_pb_t_kernel(
                     in_=xr_grouped[:, 0:I, :].rearrange("p w t -> p (w t)"),
                 )
 
-            def quantise_gu(k):
-                cols = slice(k * width, (k + 1) * width)
+            def quantise_gu():
                 nc.vector.quantize_mx(
-                    out=gu_codes[:, cols].bitcast(E5M2_X4),
-                    scales=gu_scales[:, cols],
-                    in_=gu_grouped[:, cols, :].rearrange("p w t -> p (w t)"),
+                    out=gu_codes[:].bitcast(E5M2_X4),
+                    scales=gu_scales[:],
+                    in_=gu_grouped[:].rearrange("p w t -> p (w t)"),
                 )
 
-            def products(k):
-                for m in range(k * width // P, (k + 1) * width // P):
-                    for n in range(2):
-                        if (m, n) in acc:
-                            multiply(c, m, n)
-                        else:
-                            late.append(c)
-
+            nc.vector.tensor_mul(out=gu_rows[:], in0=g_raw[:], in1=u_raw[:])
             if c == 0:
-                nc.vector.tensor_mul(out=gu_rows[:], in0=g_raw[:], in1=u_raw[:])
                 make_spread()
                 regroup(nc.vector.tensor_copy, gu_grouped[:], gu_rows[:])
-                quantise_gu(0)
+                quantise_gu()
                 quantise_rh()
                 quantise_x()
-                for h, hid_raw in hid_raws:
-                    sum_hidden(h, hid_raw)
-                products(0)
-                return
+            else:
+                quantise_rh()
+                regroup(nc.vector.tensor_copy, gu_grouped[:], gu_rows[:])
+                quantise_x()
+                quantise_gu()
+            for m in range(M_TILES):
+                for n in range(2):
+                    if (m, n) != LAST:
+                        multiply(c, m, n)
 
-            for k in range(pieces):
-                cols = slice(k * width, (k + 1) * width)
-                nc.vector.tensor_mul(out=gu_rows[:, :, cols], in0=g_raw[:, :, cols], in1=u_raw[:, :, cols])
-                if k == 0:
-                    quantise_rh()
-                    if c == GATE_PASS + 1:
-                        nc.vector.tensor_copy(out=gate_in[:], in_=gate_psum[:])
-                        acc[LAST] = psum.tile([P, N_PASS], F32, name="acc%d%d" % LAST, tag="acc%d%d" % LAST)
-                        for cc in late:
-                            multiply(cc, LAST[0], LAST[1])
-                else:
-                    quantise_gu(k - 1)
-                    products(k - 1)
-                    if k == 1:
-                        nc.vector.tensor_mul(out=cs[:], in0=gate[:], in1=gate_in[:, M_TILES : 2 * M_TILES])
-                regroup(nc.vector.tensor_copy, gu_grouped[:, cols, :], gu_rows[:, :, cols])
-                if k == 0:
-                    quantise_x()
-                    for h, hid_raw in hid_raws:
-                        sum_hidden(h, hid_raw)
-                    if c == GATE_PASS:
-                        nc.tensor.matmul(out=gate_psum[:], lhsT=vec_rows[:], rhs=spread[:], start=False, stop=True)
-            quantise_gu(pieces - 1)
-            products(pieces - 1)
+        for c in range(PASSES):
+            one_pass(c)
 
-        for c in range(PASSES - 1):
-            one_pass(c, 1)
-        one_pass(PASSES - 1, M_TILES)
+        hid_raws = []
+        for h in range(HID_CHUNKS):
+            hid_raw = hid.tile([P, HID_ROWS, H], BF16, name="hid_raw")
+            nc.sync.dma_start(out=hid_raw[:], in_=hidden_rows[:, h * HID_ROWS : (h + 1) * HID_ROWS, :])
+            hid_raws.append(hid_raw)
+        for i, h in enumerate(SUM_ORDER):
+            if h in SCALAR_CHUNKS:
+                hid_abs = hid3.tile([P, HID_ROWS, H], BF16, name="hid_abs_s")
+                nc.scalar.activation(out=hid_abs[:], in_=hid_raws[h][:], func=ACT.Abs)
+            else:
+                hid_abs = hid2.tile([P, HID_ROWS, H], BF16, name="hid_abs")
+                nc.vector.tensor_scalar(
+                    out=hid_abs[:].rearrange("p r j -> p (r j)").bitcast(I32),
+                    in0=hid_raws[h][:].rearrange("p r j -> p (r j)").bitcast(I32),
+                    scalar1=NO_SIGNS,
+                    scalar2=None,
+                    op0=ALU.bitwise_and,
+                )
+            for r in range(HID_ROWS):
+                for m in range(M_TILES):
+                    nc.tensor.matmul(
+                        out=gate_psum[:],
+                        lhsT=hid_abs[:, r, m * P : (m + 1) * P],
+                        rhs=pick[:, m, :],
+                        start=False,
+                        stop=(i == HID_CHUNKS - 1 and r == HID_ROWS - 1 and m == M_TILES - 1),
+                    )
+
+        nc.vector.tensor_copy(out=gate_in[:], in_=gate_psum[:])
+        acc[LAST] = psum.tile([P, N_PASS], F32, name="acc%d%d" % LAST, tag="acc%d%d" % LAST)
+        for c in range(PASSES):
+            multiply(c, LAST[0], LAST[1])
+        nc.scalar.activation(out=gate[:], in_=gate_in[:, 0:M_TILES], func=ACT.Sigmoid)
+        nc.vector.tensor_mul(out=cs[:], in0=gate[:], in1=gate_in[:, M_TILES : 2 * M_TILES])
 
         kept = C // 2
         for m in range(M_TILES):
@@ -267,12 +245,7 @@ def tile_persistentgrucell_pb_t_kernel(
                 func=ACT.Copy,
                 scale=cs[:, m : m + 1],
             )
-            if m < M_TILES // 2:
-                nc.scalar.activation(
-                    out=result[:, 0:kept], in_=acc[(m, 0)][:, 0:kept], func=ACT.Copy, scale=cs[:, m : m + 1]
-                )
-            else:
-                nc.vector.tensor_scalar_mul(
-                    out=result[:, 0:kept], in0=acc[(m, 0)][:, 0:kept], scalar1=cs[:, m : m + 1]
-                )
+            nc.vector.tensor_scalar_mul(
+                out=result[:, 0:kept], in0=acc[(m, 0)][:, 0:kept], scalar1=cs[:, m : m + 1]
+            )
             nc.sync.dma_start(out=out[m * P : (m + 1) * P, :], in_=result[:])

@@ -248,4 +248,8 @@ def tile_persistentgrucell_pb_t_kernel(
             nc.vector.tensor_scalar_mul(
                 out=result[:, 0:kept], in0=acc[(m, 0)][:, 0:kept], scalar1=cs[:, m : m + 1]
             )
-            nc.sync.dma_start(out=out[m * P : (m + 1) * P, :], in_=result[:])
+            if m < M_TILES - 1:
+                nc.sync.dma_start(out=out[m * P : (m + 1) * P, :], in_=result[:])
+            else:
+                nc.sync.dma_start(out=out[m * P : (m + 1) * P, 0:kept], in_=result[:, 0:kept])
+                nc.sync.dma_start(out=out[m * P : (m + 1) * P, kept:C], in_=result[:, kept:C])

@@ -23,8 +23,12 @@ M_TILES = H // P
 N_PASS = 512
 HID_CHUNKS = 8
 HID_ROWS = B // P // HID_CHUNKS
-SCALAR_CHUNKS = (0, 1)
-SUM_ORDER = (0, 2, 3, 4, 1, 5, 6, 7)
+LATE = 3
+EARLY = PASSES - LATE
+SCALAR_CHUNKS = (0, 1, 4)
+LAST_CUT = 3
+X_CUT = 160
+GATE_COLS = 48
 NO_SIGNS = 0x7FFF7FFF
 
 FLOPS = 2 * B * H * C
@@ -57,8 +61,6 @@ def tile_persistentgrucell_pb_t_kernel(
         ctx.enter_context(tc.manual_schedule())
         consts = ctx.enter_context(tc.tile_pool(name="consts", bufs=1))
         hid = ctx.enter_context(tc.tile_pool(name="hid", bufs=HID_CHUNKS))
-        hid2 = ctx.enter_context(tc.tile_pool(name="hid2", bufs=3))
-        hid3 = ctx.enter_context(tc.tile_pool(name="hid3", bufs=len(SCALAR_CHUNKS)))
         raw = ctx.enter_context(tc.tile_pool(name="raw", bufs=5))
         work = ctx.enter_context(tc.tile_pool(name="work", bufs=3))
         mx = ctx.enter_context(tc.tile_pool(name="mx", bufs=PASSES))
@@ -84,27 +86,24 @@ def tile_persistentgrucell_pb_t_kernel(
         decay_bf16 = consts.tile([M_TILES, 1], BF16)
         nc.scalar.dma_start(out=decay_bf16[:], in_=connection_decay.partition_broadcast(M_TILES))
 
-        pick = consts.tile([P, M_TILES, 2 * M_TILES], BF16)
+        pick = consts.tile([P, M_TILES, GATE_COLS], BF16)
         nc.vector.memset(pick[:], 0.0)
         for m in range(M_TILES):
             nc.vector.memset(pick[:, m, m : m + 1], 1.0 / B)
 
         hidden_rows = hidden.rearrange("(p r) j -> p r j", p=P)
-        LAST = (M_TILES - 1, 1)
-        gate_psum = psum.tile([P, 2 * M_TILES], F32, name="gate_psum", tag="acc%d%d" % LAST)
-        spread = consts.tile([P, 2 * M_TILES], BF16)
-        gate_in = consts.tile([P, 2 * M_TILES], F32)
+        LAST = (M_TILES - 1, 0)
+        spread = consts.tile([P, GATE_COLS], BF16)
         gate = consts.tile([P, M_TILES], F32)
         cs = consts.tile([P, M_TILES], F32)
 
         def make_spread():
             decay = consts.tile([M_TILES, 1], F32)
             nc.vector.tensor_copy(out=decay[:], in_=decay_bf16[:])
-            nc.vector.tensor_copy(out=spread[:], in_=identity[:, 0 : 2 * M_TILES])
+            nc.vector.tensor_copy(out=spread[:], in_=identity[:, 0:GATE_COLS])
             nc.vector.tensor_scalar_mul(
                 out=spread[0:M_TILES, 0:M_TILES], in0=identity[0:M_TILES, 0:M_TILES], scalar1=decay[:, 0:1]
             )
-            nc.tensor.matmul(out=gate_psum[:], lhsT=vec_rows[:], rhs=spread[:], start=True, stop=False)
 
         g_passes = grad_out.rearrange("(c p t) j -> c p t j", p=P, t=PACK)
         u_passes = update.rearrange("(c p t) j -> c p t j", p=P, t=PACK)
@@ -115,8 +114,7 @@ def tile_persistentgrucell_pb_t_kernel(
         acc = {}
         for m in range(M_TILES):
             for n in range(2):
-                if (m, n) != LAST:
-                    acc[(m, n)] = psum.tile([P, N_PASS], F32, name="acc%d%d" % (m, n), tag="acc%d%d" % (m, n))
+                acc[(m, n)] = psum.tile([P, N_PASS], F32, name="acc%d%d" % (m, n), tag="acc%d%d" % (m, n))
         codes = {}
 
         def multiply(c, m, n):
@@ -127,29 +125,47 @@ def tile_persistentgrucell_pb_t_kernel(
                 lhsT_scale=gu_scales[:, m * P : (m + 1) * P],
                 rhs=xr_codes[:, windows[n]].bitcast(E4M3_X4),
                 rhs_scale=xr_scales[:, windows[n]],
-                start=(c == 0),
-                stop=(c == PASSES - 1),
+                start=(c == 0 or (c == EARLY and (m, n) == LAST)),
+                stop=(c == PASSES - 1 or (c == EARLY - 1 and (m, n) == LAST)),
             )
+
+        def regroup_x(copy, c, x_raw):
+            x_grouped = work.tile([P, I, PACK], BF16, name="x_grouped", align_bytes=64)
+            regroup(copy, x_grouped[:], x_raw[:])
+            return x_grouped
+
+        def quantise_x(c, x_grouped):
+            nc.vector.quantize_mx(
+                out=codes[c][2][:, 0:I].bitcast(E4M3_X4),
+                scales=codes[c][3][:, 0:I],
+                in_=x_grouped[:].rearrange("p w t -> p (w t)"),
+            )
+
+        def load_x(c):
+            x_raw = raw.tile([P, PACK, I], BF16, name="x_raw")
+            nc.sync.dma_start(out=x_raw[:], in_=x_passes[c])
+            return x_raw
 
         def one_pass(c):
             rh_raw = raw.tile([P, PACK, H], BF16, name="rh_raw")
-            x_raw = raw.tile([P, PACK, I], BF16, name="x_raw")
             g_raw = raw.tile([P, PACK, H], BF16, name="g_raw")
             u_raw = raw.tile([P, PACK, H], BF16, name="u_raw")
             if c == 0:
                 nc.sync.dma_start(out=g_raw[:], in_=g_passes[c])
                 nc.sync.dma_start(out=u_raw[:], in_=u_passes[c])
                 nc.sync.dma_start(out=rh_raw[:], in_=rh_passes[c])
-                nc.sync.dma_start(out=x_raw[:], in_=x_passes[c])
+                x_raw = load_x(c)
             else:
                 nc.sync.dma_start(out=rh_raw[:], in_=rh_passes[c])
-                nc.sync.dma_start(out=x_raw[:], in_=x_passes[c])
+                if c < EARLY:
+                    x_raw = load_x(c)
                 nc.sync.dma_start(out=g_raw[:], in_=g_passes[c])
                 nc.sync.dma_start(out=u_raw[:], in_=u_passes[c])
 
-            xr_grouped = work.tile([P, C, PACK], BF16, name="xr_grouped", align_bytes=64)
-            regroup(nc.scalar.copy, xr_grouped[:, I:C, :], rh_raw[:])
-            regroup(nc.scalar.copy, xr_grouped[:, 0:I, :], x_raw[:])
+            rh_grouped = work.tile([P, H, PACK], BF16, name="rh_grouped", align_bytes=64)
+            regroup(nc.scalar.copy, rh_grouped[:], rh_raw[:])
+            if c < EARLY:
+                x_grouped = regroup_x(nc.scalar.copy, c, x_raw)
 
             gu_codes = mx.tile([P, H], U32, name="gu_codes", align_bytes=64)
             gu_scales = mx.tile([P, H], U8, name="gu_scales", align_bytes=64)
@@ -164,14 +180,7 @@ def tile_persistentgrucell_pb_t_kernel(
                 nc.vector.quantize_mx(
                     out=xr_codes[:, I:C].bitcast(E4M3_X4),
                     scales=xr_scales[:, I:C],
-                    in_=xr_grouped[:, I:C, :].rearrange("p w t -> p (w t)"),
-                )
-
-            def quantise_x():
-                nc.vector.quantize_mx(
-                    out=xr_codes[:, 0:I].bitcast(E4M3_X4),
-                    scales=xr_scales[:, 0:I],
-                    in_=xr_grouped[:, 0:I, :].rearrange("p w t -> p (w t)"),
+                    in_=rh_grouped[:].rearrange("p w t -> p (w t)"),
                 )
 
             def quantise_gu():
@@ -187,69 +196,118 @@ def tile_persistentgrucell_pb_t_kernel(
                 regroup(nc.vector.tensor_copy, gu_grouped[:], gu_rows[:])
                 quantise_gu()
                 quantise_rh()
-                quantise_x()
+                quantise_x(c, x_grouped)
             else:
                 quantise_rh()
                 regroup(nc.vector.tensor_copy, gu_grouped[:], gu_rows[:])
-                quantise_x()
+                if c < EARLY:
+                    quantise_x(c, x_grouped)
                 quantise_gu()
             for m in range(M_TILES):
                 for n in range(2):
-                    if (m, n) != LAST:
+                    if n == 1 or c < EARLY:
                         multiply(c, m, n)
 
         for c in range(PASSES):
             one_pass(c)
+
+        partial = consts.tile([P, I], F32)
+        nc.scalar.copy(out=partial[:], in_=acc[LAST][:, 0:I])
+        gate_psum = psum.tile([P, GATE_COLS], F32, name="gate_psum", tag="acc%d%d" % LAST)
 
         hid_raws = []
         for h in range(HID_CHUNKS):
             hid_raw = hid.tile([P, HID_ROWS, H], BF16, name="hid_raw")
             nc.sync.dma_start(out=hid_raw[:], in_=hidden_rows[:, h * HID_ROWS : (h + 1) * HID_ROWS, :])
             hid_raws.append(hid_raw)
-        for i, h in enumerate(SUM_ORDER):
-            if h in SCALAR_CHUNKS:
-                hid_abs = hid3.tile([P, HID_ROWS, H], BF16, name="hid_abs_s")
-                nc.scalar.activation(out=hid_abs[:], in_=hid_raws[h][:], func=ACT.Abs)
+        x_raws = {}
+        for c in range(EARLY, PASSES):
+            x_raws[c] = load_x(c)
+
+        nc.tensor.matmul(out=gate_psum[:], lhsT=vec_rows[:], rhs=spread[:], start=True, stop=False)
+
+        def clear_signs(part):
+            words = part.rearrange("p r j -> p (r j)").bitcast(I32)
+            nc.vector.tensor_scalar(out=words, in0=words, scalar1=NO_SIGNS, scalar2=None, op0=ALU.bitwise_and)
+
+        def absolute(part):
+            nc.scalar.activation(out=part, in_=part, func=ACT.Abs)
+
+        for h in range(HID_CHUNKS):
+            chunk = hid_raws[h]
+            if h == HID_CHUNKS - 1:
+                clear_signs(chunk[:, 0:LAST_CUT, :])
+                absolute(chunk[:, LAST_CUT:HID_ROWS, :])
+            elif h in SCALAR_CHUNKS:
+                absolute(chunk[:])
             else:
-                hid_abs = hid2.tile([P, HID_ROWS, H], BF16, name="hid_abs")
-                nc.vector.tensor_scalar(
-                    out=hid_abs[:].rearrange("p r j -> p (r j)").bitcast(I32),
-                    in0=hid_raws[h][:].rearrange("p r j -> p (r j)").bitcast(I32),
-                    scalar1=NO_SIGNS,
-                    scalar2=None,
-                    op0=ALU.bitwise_and,
-                )
+                clear_signs(chunk[:])
             for r in range(HID_ROWS):
                 for m in range(M_TILES):
                     nc.tensor.matmul(
                         out=gate_psum[:],
-                        lhsT=hid_abs[:, r, m * P : (m + 1) * P],
+                        lhsT=chunk[:, r, m * P : (m + 1) * P],
                         rhs=pick[:, m, :],
                         start=False,
-                        stop=(i == HID_CHUNKS - 1 and r == HID_ROWS - 1 and m == M_TILES - 1),
+                        stop=(h == HID_CHUNKS - 1 and r == HID_ROWS - 1 and m == M_TILES - 1),
                     )
 
-        nc.vector.tensor_copy(out=gate_in[:], in_=gate_psum[:])
-        acc[LAST] = psum.tile([P, N_PASS], F32, name="acc%d%d" % LAST, tag="acc%d%d" % LAST)
-        for c in range(PASSES):
-            multiply(c, LAST[0], LAST[1])
-        nc.scalar.activation(out=gate[:], in_=gate_in[:, 0:M_TILES], func=ACT.Sigmoid)
-        nc.vector.tensor_mul(out=cs[:], in0=gate[:], in1=gate_in[:, M_TILES : 2 * M_TILES])
+        def regroup_late(c):
+            x_grouped = work.tile([P, I, PACK], BF16, name="x_grouped", align_bytes=64)
+            regroup(nc.vector.tensor_copy, x_grouped[:, 0:X_CUT, :], x_raws[c][:, :, 0:X_CUT])
+            regroup(nc.scalar.copy, x_grouped[:, X_CUT:I, :], x_raws[c][:, :, X_CUT:I])
+            return x_grouped
 
-        kept = C // 2
+        c5, c6, c7 = range(EARLY, PASSES)
+        x5_grouped = regroup_late(c5)
+        quantise_x(c5, x5_grouped)
+        for m in range(M_TILES - 1):
+            multiply(c5, m, 0)
+        nc.scalar.activation(out=gate[:], in_=gate_psum[:, 0:M_TILES], func=ACT.Sigmoid)
+        nc.vector.tensor_mul(out=cs[:], in0=gate[:], in1=gate_psum[:, M_TILES : 2 * M_TILES])
+        acc[LAST] = psum.tile([P, N_PASS], F32, name="acc%d%d" % LAST, tag="acc%d%d" % LAST)
+        multiply(c5, *LAST)
+
+        def scale_on_scalar(dst, src, m):
+            nc.scalar.activation(out=dst, in_=src, func=ACT.Copy, scale=cs[:, m : m + 1])
+
+        def scale_on_vector(dst, src, m):
+            nc.vector.tensor_scalar_mul(out=dst, in0=src, scalar1=cs[:, m : m + 1])
+
+        def rh_out(m, cut):
+            rh_result = results.tile([P, H], F32, name="rh_result")
+            if cut > 0:
+                scale_on_vector(rh_result[:, 0:cut], acc[(m, 1)][:, 0:cut], m)
+            scale_on_scalar(rh_result[:, cut:H], acc[(m, 1)][:, cut:H], m)
+            nc.sync.dma_start(out=out[m * P : (m + 1) * P, I:C], in_=rh_result[:])
+
+        rh_out(0, H // 2)
+        x6_grouped = regroup_late(c6)
+        rh_out(1, H // 2)
+        quantise_x(c6, x6_grouped)
         for m in range(M_TILES):
-            result = results.tile([P, C], F32)
-            nc.scalar.activation(
-                out=result[:, kept:C],
-                in_=acc[(m, 1)][:, N_PASS - kept : N_PASS],
-                func=ACT.Copy,
-                scale=cs[:, m : m + 1],
-            )
-            nc.vector.tensor_scalar_mul(
-                out=result[:, 0:kept], in0=acc[(m, 0)][:, 0:kept], scalar1=cs[:, m : m + 1]
-            )
-            if m < M_TILES - 1:
-                nc.sync.dma_start(out=out[m * P : (m + 1) * P, :], in_=result[:])
+            multiply(c6, m, 0)
+        x7_grouped = regroup_late(c7)
+        rh_out(2, H // 2)
+        quantise_x(c7, x7_grouped)
+        for m in range(M_TILES):
+            multiply(c7, m, 0)
+        rh_out(3, H // 2)
+        scale_on_scalar(partial[:], partial[:], M_TILES - 1)
+
+        for m in range(M_TILES):
+            x_result = results.tile([P, I], F32, name="x_result")
+            if m == M_TILES - 1:
+                nc.vector.scalar_tensor_tensor(
+                    out=x_result[:],
+                    in0=acc[LAST][:, 0:I],
+                    scalar=cs[:, m : m + 1],
+                    in1=partial[:],
+                    op0=ALU.mult,
+                    op1=ALU.add,
+                )
+            elif m % 2 == 0:
+                scale_on_scalar(x_result[:], acc[(m, 0)][:, 0:I], m)
             else:
-                nc.sync.dma_start(out=out[m * P : (m + 1) * P, 0:kept], in_=result[:, 0:kept])
-                nc.sync.dma_start(out=out[m * P : (m + 1) * P, kept:C], in_=result[:, kept:C])
+                scale_on_vector(x_result[:], acc[(m, 0)][:, 0:I], m)
+            nc.sync.dma_start(out=out[m * P : (m + 1) * P, 0:I], in_=x_result[:])

@@ -21,13 +21,11 @@ K_PASS = P * PACK
 PASSES = B // K_PASS
 M_TILES = H // P
 N_PASS = 512
-HID_CHUNKS = 8
-HID_ROWS = B // P // HID_CHUNKS
+HID_ROWS = (4, 4, 4, 4, 4, 4, 4, 2, 2)
 LATE = 3
 EARLY = PASSES - LATE
-SCALAR_CHUNKS = (0, 1, 4)
-LAST_CUT = 3
-X_CUT = 160
+SCALAR_CHUNKS = (0, 1)
+X_CUTS = (192, 96, 96)
 GATE_COLS = 48
 NO_SIGNS = 0x7FFF7FFF
 
@@ -60,7 +58,7 @@ def tile_persistentgrucell_pb_t_kernel(
     with ExitStack() as ctx:
         ctx.enter_context(tc.manual_schedule())
         consts = ctx.enter_context(tc.tile_pool(name="consts", bufs=1))
-        hid = ctx.enter_context(tc.tile_pool(name="hid", bufs=HID_CHUNKS))
+        hid = ctx.enter_context(tc.tile_pool(name="hid", bufs=1))
         raw = ctx.enter_context(tc.tile_pool(name="raw", bufs=5))
         work = ctx.enter_context(tc.tile_pool(name="work", bufs=3))
         mx = ctx.enter_context(tc.tile_pool(name="mx", bufs=PASSES))
@@ -203,6 +201,8 @@ def tile_persistentgrucell_pb_t_kernel(
                 if c < EARLY:
                     quantise_x(c, x_grouped)
                 quantise_gu()
+
+        def products(c):
             for m in range(M_TILES):
                 for n in range(2):
                     if n == 1 or c < EARLY:
@@ -210,16 +210,20 @@ def tile_persistentgrucell_pb_t_kernel(
 
         for c in range(PASSES):
             one_pass(c)
+            if c < PASSES - 1:
+                products(c)
 
         partial = consts.tile([P, I], F32)
         nc.scalar.copy(out=partial[:], in_=acc[LAST][:, 0:I])
         gate_psum = psum.tile([P, GATE_COLS], F32, name="gate_psum", tag="acc%d%d" % LAST)
 
         hid_raws = []
-        for h in range(HID_CHUNKS):
-            hid_raw = hid.tile([P, HID_ROWS, H], BF16, name="hid_raw")
-            nc.sync.dma_start(out=hid_raw[:], in_=hidden_rows[:, h * HID_ROWS : (h + 1) * HID_ROWS, :])
+        first_row = 0
+        for h, rows in enumerate(HID_ROWS):
+            hid_raw = hid.tile([P, rows, H], BF16, name="hid_raw%d" % h)
+            nc.sync.dma_start(out=hid_raw[:], in_=hidden_rows[:, first_row : first_row + rows, :])
             hid_raws.append(hid_raw)
+            first_row += rows
         x_raws = {}
         for c in range(EARLY, PASSES):
             x_raws[c] = load_x(c)
@@ -233,40 +237,47 @@ def tile_persistentgrucell_pb_t_kernel(
         def absolute(part):
             nc.scalar.activation(out=part, in_=part, func=ACT.Abs)
 
-        for h in range(HID_CHUNKS):
+        for h, rows in enumerate(HID_ROWS):
             chunk = hid_raws[h]
-            if h == HID_CHUNKS - 1:
-                clear_signs(chunk[:, 0:LAST_CUT, :])
-                absolute(chunk[:, LAST_CUT:HID_ROWS, :])
-            elif h in SCALAR_CHUNKS:
+            if h in SCALAR_CHUNKS:
                 absolute(chunk[:])
             else:
                 clear_signs(chunk[:])
-            for r in range(HID_ROWS):
+            if h == 1:
+                products(PASSES - 1)
+            for r in range(rows):
                 for m in range(M_TILES):
                     nc.tensor.matmul(
                         out=gate_psum[:],
                         lhsT=chunk[:, r, m * P : (m + 1) * P],
                         rhs=pick[:, m, :],
                         start=False,
-                        stop=(h == HID_CHUNKS - 1 and r == HID_ROWS - 1 and m == M_TILES - 1),
+                        stop=(h == len(HID_ROWS) - 1 and r == rows - 1 and m == M_TILES - 1),
                     )
 
-        def regroup_late(c):
+        rh_results = []
+        for m in range(M_TILES):
+            rh_result = results.tile([P, H], F32, name="rh_result")
+            nc.scalar.copy(out=rh_result[:], in_=acc[(m, 1)][:])
+            rh_results.append(rh_result)
+
+        def regroup_late(k):
             x_grouped = work.tile([P, I, PACK], BF16, name="x_grouped", align_bytes=64)
-            regroup(nc.vector.tensor_copy, x_grouped[:, 0:X_CUT, :], x_raws[c][:, :, 0:X_CUT])
-            regroup(nc.scalar.copy, x_grouped[:, X_CUT:I, :], x_raws[c][:, :, X_CUT:I])
+            x_raw = x_raws[late[k]]
+            cut = X_CUTS[k]
+            regroup(nc.vector.tensor_copy, x_grouped[:, 0:cut, :], x_raw[:, :, 0:cut])
+            regroup(nc.scalar.copy, x_grouped[:, cut:I, :], x_raw[:, :, cut:I])
             return x_grouped
 
-        c5, c6, c7 = range(EARLY, PASSES)
-        x5_grouped = regroup_late(c5)
-        quantise_x(c5, x5_grouped)
+        late = list(range(EARLY, PASSES))
+        x_grouped = regroup_late(0)
+        quantise_x(late[0], x_grouped)
         for m in range(M_TILES - 1):
-            multiply(c5, m, 0)
+            multiply(late[0], m, 0)
         nc.scalar.activation(out=gate[:], in_=gate_psum[:, 0:M_TILES], func=ACT.Sigmoid)
         nc.vector.tensor_mul(out=cs[:], in0=gate[:], in1=gate_psum[:, M_TILES : 2 * M_TILES])
         acc[LAST] = psum.tile([P, N_PASS], F32, name="acc%d%d" % LAST, tag="acc%d%d" % LAST)
-        multiply(c5, *LAST)
+        multiply(late[0], *LAST)
 
         def scale_on_scalar(dst, src, m):
             nc.scalar.activation(out=dst, in_=src, func=ACT.Copy, scale=cs[:, m : m + 1])
@@ -274,25 +285,16 @@ def tile_persistentgrucell_pb_t_kernel(
         def scale_on_vector(dst, src, m):
             nc.vector.tensor_scalar_mul(out=dst, in0=src, scalar1=cs[:, m : m + 1])
 
-        def rh_out(m, cut):
-            rh_result = results.tile([P, H], F32, name="rh_result")
-            if cut > 0:
-                scale_on_vector(rh_result[:, 0:cut], acc[(m, 1)][:, 0:cut], m)
-            scale_on_scalar(rh_result[:, cut:H], acc[(m, 1)][:, cut:H], m)
+        for m in range(M_TILES):
+            rh_result = rh_results[m]
+            scale_on_vector(rh_result[:], rh_result[:], m)
             nc.sync.dma_start(out=out[m * P : (m + 1) * P, I:C], in_=rh_result[:])
-
-        rh_out(0, H // 2)
-        x6_grouped = regroup_late(c6)
-        rh_out(1, H // 2)
-        quantise_x(c6, x6_grouped)
-        for m in range(M_TILES):
-            multiply(c6, m, 0)
-        x7_grouped = regroup_late(c7)
-        rh_out(2, H // 2)
-        quantise_x(c7, x7_grouped)
-        for m in range(M_TILES):
-            multiply(c7, m, 0)
-        rh_out(3, H // 2)
+            if 1 <= m < LATE:
+                quantise_x(late[m], x_grouped)
+                for n in range(M_TILES):
+                    multiply(late[m], n, 0)
+            if m + 1 < LATE:
+                x_grouped = regroup_late(m + 1)
         scale_on_scalar(partial[:], partial[:], M_TILES - 1)
 
         for m in range(M_TILES):

@@ -21,7 +21,7 @@ K_PASS = P * PACK
 PASSES = B // K_PASS
 M_TILES = H // P
 N_PASS = 512
-HID_ROWS = (4, 4, 4, 4, 4, 4, 4, 2, 2)
+HID_ROWS = (4, 4, 4, 4, 4, 4, 4, 2, 1, 1)
 LATE = 3
 EARLY = PASSES - LATE
 SCALAR_CHUNKS = (0, 1)

@@ -24,7 +24,8 @@ N_PASS = 512
 HID_ROWS = (4, 4, 4, 4, 4, 4, 4, 2, 1, 1)
 LATE = 3
 EARLY = PASSES - LATE
-SCALAR_CHUNKS = (0, 1)
+SUM_ORDER = (1, 2, 0, 3, 4, 5, 6, 7, 8, 9)
+GU_CUT = 320
 X_CUTS = (192, 96, 96)
 GATE_COLS = 48
 NO_SIGNS = 0x7FFF7FFF
@@ -197,9 +198,12 @@ def tile_persistentgrucell_pb_t_kernel(
                 quantise_x(c, x_grouped)
             else:
                 quantise_rh()
-                regroup(nc.vector.tensor_copy, gu_grouped[:], gu_rows[:])
                 if c < EARLY:
+                    regroup(nc.vector.tensor_copy, gu_grouped[:], gu_rows[:])
                     quantise_x(c, x_grouped)
+                else:
+                    regroup(nc.vector.tensor_copy, gu_grouped[:, 0:GU_CUT, :], gu_rows[:, :, 0:GU_CUT])
+                    regroup(nc.scalar.copy, gu_grouped[:, GU_CUT:H, :], gu_rows[:, :, GU_CUT:H])
                 quantise_gu()
 
         def products(c):
@@ -237,29 +241,25 @@ def tile_persistentgrucell_pb_t_kernel(
         def absolute(part):
             nc.scalar.activation(out=part, in_=part, func=ACT.Abs)
 
-        for h, rows in enumerate(HID_ROWS):
-            chunk = hid_raws[h]
-            if h in SCALAR_CHUNKS:
-                absolute(chunk[:])
-            else:
-                clear_signs(chunk[:])
-            if h == 1:
-                products(PASSES - 1)
-            for r in range(rows):
-                for m in range(M_TILES):
-                    nc.tensor.matmul(
-                        out=gate_psum[:],
-                        lhsT=chunk[:, r, m * P : (m + 1) * P],
-                        rhs=pick[:, m, :],
-                        start=False,
-                        stop=(h == len(HID_ROWS) - 1 and r == rows - 1 and m == M_TILES - 1),
-                    )
-
+        products(PASSES - 1)
+        absolute(hid_raws[0][:])
         rh_results = []
         for m in range(M_TILES):
             rh_result = results.tile([P, H], F32, name="rh_result")
             nc.scalar.copy(out=rh_result[:], in_=acc[(m, 1)][:])
             rh_results.append(rh_result)
+        for hid_raw in hid_raws[1:]:
+            clear_signs(hid_raw[:])
+        for h in SUM_ORDER:
+            for r in range(HID_ROWS[h]):
+                for m in range(M_TILES):
+                    nc.tensor.matmul(
+                        out=gate_psum[:],
+                        lhsT=hid_raws[h][:, r, m * P : (m + 1) * P],
+                        rhs=pick[:, m, :],
+                        start=False,
+                        stop=(h == SUM_ORDER[-1] and r == HID_ROWS[h] - 1 and m == M_TILES - 1),
+                    )
 
         def regroup_late(k):
             x_grouped = work.tile([P, I, PACK], BF16, name="x_grouped", align_bytes=64)

@@ -27,7 +27,7 @@ EARLY = PASSES - LATE
 SUM_ORDER = (1, 2, 0, 3, 4, 5, 6, 7, 8, 9)
 GU_CUT = 320
 X_CUTS = (192, 96, 96)
-GATE_COLS = 48
+GATE_COLS = 72
 NO_SIGNS = 0x7FFF7FFF
 
 FLOPS = 2 * B * H * C

@@ -24,9 +24,10 @@ N_PASS = 512
 HID_ROWS = (4, 4, 4, 4, 4, 4, 4, 2, 1, 1)
 LATE = 3
 EARLY = PASSES - LATE
-SUM_ORDER = (1, 2, 0, 3, 4, 5, 6, 7, 8, 9)
 GU_CUT = 320
-X_CUTS = (192, 96, 96)
+X_CUTS = (160, 96, 96)
+DENSE_LOADS = 5
+DENSE_COLS = 32
 GATE_COLS = 72
 NO_SIGNS = 0x7FFF7FFF
 
@@ -145,6 +146,46 @@ def tile_persistentgrucell_pb_t_kernel(
             nc.sync.dma_start(out=x_raw[:], in_=x_passes[c])
             return x_raw
 
+        hid_raws = []
+        x_raws = {}
+        partial = consts.tile([P, I], F32)
+        gates = []
+
+        def load_hidden_and_late_x():
+            first_row = 0
+            for h, rows in enumerate(HID_ROWS):
+                hid_raw = hid.tile([P, rows, H], BF16, name="hid_raw%d" % h)
+                nc.sync.dma_start(out=hid_raw[:], in_=hidden_rows[:, first_row : first_row + rows, :])
+                hid_raws.append(hid_raw)
+                first_row += rows
+            for c in range(EARLY, PASSES):
+                x_raws[c] = load_x(c)
+
+        def open_gate():
+            nc.scalar.copy(out=partial[:], in_=acc[LAST][:, 0:I])
+            gate_psum = psum.tile([P, GATE_COLS], F32, name="gate_psum", tag="acc%d%d" % LAST)
+            nc.tensor.matmul(out=gate_psum[:], lhsT=vec_rows[:], rhs=spread[:], start=True, stop=False)
+            gates.append(gate_psum)
+
+        def clear_signs(part):
+            words = part.rearrange("p r j -> p (r j)").bitcast(I32)
+            nc.vector.tensor_scalar(out=words, in0=words, scalar1=NO_SIGNS, scalar2=None, op0=ALU.bitwise_and)
+
+        def absolute(part):
+            nc.scalar.activation(out=part, in_=part, func=ACT.Abs)
+
+        def gate_sums(h):
+            cols = DENSE_COLS if h < DENSE_LOADS else GATE_COLS
+            for r in range(HID_ROWS[h]):
+                for m in range(M_TILES):
+                    nc.tensor.matmul(
+                        out=gates[0][:, 0:cols],
+                        lhsT=hid_raws[h][:, r, m * P : (m + 1) * P],
+                        rhs=pick[:, m, 0:cols],
+                        start=False,
+                        stop=(h == len(HID_ROWS) - 1 and r == HID_ROWS[h] - 1 and m == M_TILES - 1),
+                    )
+
         def one_pass(c):
             rh_raw = raw.tile([P, PACK, H], BF16, name="rh_raw")
             g_raw = raw.tile([P, PACK, H], BF16, name="g_raw")
@@ -160,6 +201,10 @@ def tile_persistentgrucell_pb_t_kernel(
                     x_raw = load_x(c)
                 nc.sync.dma_start(out=g_raw[:], in_=g_passes[c])
                 nc.sync.dma_start(out=u_raw[:], in_=u_passes[c])
+
+            if c == PASSES - 1:
+                load_hidden_and_late_x()
+                open_gate()
 
             rh_grouped = work.tile([P, H, PACK], BF16, name="rh_grouped", align_bytes=64)
             regroup(nc.scalar.copy, rh_grouped[:], rh_raw[:])
@@ -190,6 +235,9 @@ def tile_persistentgrucell_pb_t_kernel(
                 )
 
             nc.vector.tensor_mul(out=gu_rows[:], in0=g_raw[:], in1=u_raw[:])
+            if c == PASSES - 1:
+                clear_signs(hid_raws[0][:])
+                gate_sums(0)
             if c == 0:
                 make_spread()
                 regroup(nc.vector.tensor_copy, gu_grouped[:], gu_rows[:])
@@ -214,52 +262,19 @@ def tile_persistentgrucell_pb_t_kernel(
 
         for c in range(PASSES):
             one_pass(c)
-            if c < PASSES - 1:
-                products(c)
+            products(c)
 
-        partial = consts.tile([P, I], F32)
-        nc.scalar.copy(out=partial[:], in_=acc[LAST][:, 0:I])
-        gate_psum = psum.tile([P, GATE_COLS], F32, name="gate_psum", tag="acc%d%d" % LAST)
-
-        hid_raws = []
-        first_row = 0
-        for h, rows in enumerate(HID_ROWS):
-            hid_raw = hid.tile([P, rows, H], BF16, name="hid_raw%d" % h)
-            nc.sync.dma_start(out=hid_raw[:], in_=hidden_rows[:, first_row : first_row + rows, :])
-            hid_raws.append(hid_raw)
-            first_row += rows
-        x_raws = {}
-        for c in range(EARLY, PASSES):
-            x_raws[c] = load_x(c)
-
-        nc.tensor.matmul(out=gate_psum[:], lhsT=vec_rows[:], rhs=spread[:], start=True, stop=False)
-
-        def clear_signs(part):
-            words = part.rearrange("p r j -> p (r j)").bitcast(I32)
-            nc.vector.tensor_scalar(out=words, in0=words, scalar1=NO_SIGNS, scalar2=None, op0=ALU.bitwise_and)
-
-        def absolute(part):
-            nc.scalar.activation(out=part, in_=part, func=ACT.Abs)
-
-        products(PASSES - 1)
-        absolute(hid_raws[0][:])
+        absolute(hid_raws[1][:])
         rh_results = []
         for m in range(M_TILES):
             rh_result = results.tile([P, H], F32, name="rh_result")
             nc.scalar.copy(out=rh_result[:], in_=acc[(m, 1)][:])
             rh_results.append(rh_result)
-        for hid_raw in hid_raws[1:]:
-            clear_signs(hid_raw[:])
-        for h in SUM_ORDER:
-            for r in range(HID_ROWS[h]):
-                for m in range(M_TILES):
-                    nc.tensor.matmul(
-                        out=gate_psum[:],
-                        lhsT=hid_raws[h][:, r, m * P : (m + 1) * P],
-                        rhs=pick[:, m, :],
-                        start=False,
-                        stop=(h == SUM_ORDER[-1] and r == HID_ROWS[h] - 1 and m == M_TILES - 1),
-                    )
+        for h in range(1, len(HID_ROWS)):
+            if h > 1:
+                clear_signs(hid_raws[h][:])
+            gate_sums(h)
+        gate_psum = gates[0]
 
         def regroup_late(k):
             x_grouped = work.tile([P, I, PACK], BF16, name="x_grouped", align_bytes=64)
@@ -287,7 +302,10 @@ def tile_persistentgrucell_pb_t_kernel(
 
         for m in range(M_TILES):
             rh_result = rh_results[m]
-            scale_on_vector(rh_result[:], rh_result[:], m)
+            if m % 2 == 0:
+                scale_on_vector(rh_result[:], rh_result[:], m)
+            else:
+                scale_on_scalar(rh_result[:], rh_result[:], m)
             nc.sync.dma_start(out=out[m * P : (m + 1) * P, I:C], in_=rh_result[:])
             if 1 <= m < LATE:
                 quantise_x(late[m], x_grouped)

@@ -25,7 +25,8 @@ HID_ROWS = (4, 4, 4, 4, 4, 4, 4, 2, 1, 1)
 LATE = 3
 EARLY = PASSES - LATE
 GU_CUT = 320
-X_CUTS = (160, 96, 96)
+X_LEAD = 2
+X_CUT = 160
 DENSE_LOADS = 5
 DENSE_COLS = 32
 GATE_COLS = 72
@@ -158,7 +159,9 @@ def tile_persistentgrucell_pb_t_kernel(
                 nc.sync.dma_start(out=hid_raw[:], in_=hidden_rows[:, first_row : first_row + rows, :])
                 hid_raws.append(hid_raw)
                 first_row += rows
-            for c in range(EARLY, PASSES):
+                if h == len(HID_ROWS) - 1 - X_LEAD:
+                    x_raws[EARLY] = load_x(EARLY)
+            for c in range(EARLY + 1, PASSES):
                 x_raws[c] = load_x(c)
 
         def open_gate():
@@ -270,29 +273,15 @@ def tile_persistentgrucell_pb_t_kernel(
             rh_result = results.tile([P, H], F32, name="rh_result")
             nc.scalar.copy(out=rh_result[:], in_=acc[(m, 1)][:])
             rh_results.append(rh_result)
-        for h in range(1, len(HID_ROWS)):
-            if h > 1:
-                clear_signs(hid_raws[h][:])
-            gate_sums(h)
-        gate_psum = gates[0]
 
-        def regroup_late(k):
-            x_grouped = work.tile([P, I, PACK], BF16, name="x_grouped", align_bytes=64)
-            x_raw = x_raws[late[k]]
-            cut = X_CUTS[k]
-            regroup(nc.vector.tensor_copy, x_grouped[:, 0:cut, :], x_raw[:, :, 0:cut])
-            regroup(nc.scalar.copy, x_grouped[:, cut:I, :], x_raw[:, :, cut:I])
-            return x_grouped
+        x_grouped = {}
 
-        late = list(range(EARLY, PASSES))
-        x_grouped = regroup_late(0)
-        quantise_x(late[0], x_grouped)
-        for m in range(M_TILES - 1):
-            multiply(late[0], m, 0)
-        nc.scalar.activation(out=gate[:], in_=gate_psum[:, 0:M_TILES], func=ACT.Sigmoid)
-        nc.vector.tensor_mul(out=cs[:], in0=gate[:], in1=gate_psum[:, M_TILES : 2 * M_TILES])
-        acc[LAST] = psum.tile([P, N_PASS], F32, name="acc%d%d" % LAST, tag="acc%d%d" % LAST)
-        multiply(late[0], *LAST)
+        def regroup_on_vector(c):
+            x_grouped[c] = work.tile([P, I, PACK], BF16, name="x_grouped", align_bytes=64)
+            regroup(nc.vector.tensor_copy, x_grouped[c][:, 0:X_CUT, :], x_raws[c][:, :, 0:X_CUT])
+
+        def regroup_on_scalar(c):
+            regroup(nc.scalar.copy, x_grouped[c][:, X_CUT:I, :], x_raws[c][:, :, X_CUT:I])
 
         def scale_on_scalar(dst, src, m):
             nc.scalar.activation(out=dst, in_=src, func=ACT.Copy, scale=cs[:, m : m + 1])
@@ -300,19 +289,41 @@ def tile_persistentgrucell_pb_t_kernel(
         def scale_on_vector(dst, src, m):
             nc.vector.tensor_scalar_mul(out=dst, in0=src, scalar1=cs[:, m : m + 1])
 
+        def rh_out(scale, m):
+            scale(rh_results[m][:], rh_results[m][:], m)
+            nc.sync.dma_start(out=out[m * P : (m + 1) * P, I:C], in_=rh_results[m][:])
+
+        c5, c6, c7 = range(EARLY, PASSES)
+        for h in range(1, len(HID_ROWS)):
+            if h == len(HID_ROWS) - X_LEAD:
+                regroup_on_vector(c5)
+                regroup_on_scalar(c5)
+            if h > 1:
+                clear_signs(hid_raws[h][:])
+            gate_sums(h)
+        gate_psum = gates[0]
+        quantise_x(c5, x_grouped[c5])
+        for m in range(M_TILES - 1):
+            multiply(c5, m, 0)
+        regroup_on_vector(c6)
+        nc.scalar.activation(out=gate[:], in_=gate_psum[:, 0:M_TILES], func=ACT.Sigmoid)
+        nc.vector.tensor_mul(out=cs[:], in0=gate[:], in1=gate_psum[:, M_TILES : 2 * M_TILES])
+        acc[LAST] = psum.tile([P, N_PASS], F32, name="acc%d%d" % LAST, tag="acc%d%d" % LAST)
+        regroup_on_scalar(c6)
+        rh_out(scale_on_vector, 0)
+        quantise_x(c6, x_grouped[c6])
+        for m in range(M_TILES - 1):
+            multiply(c6, m, 0)
+        multiply(c5, *LAST)
+        multiply(c6, *LAST)
+        regroup_on_vector(c7)
+        regroup_on_scalar(c7)
+        rh_out(scale_on_scalar, 1)
+        quantise_x(c7, x_grouped[c7])
         for m in range(M_TILES):
-            rh_result = rh_results[m]
-            if m % 2 == 0:
-                scale_on_vector(rh_result[:], rh_result[:], m)
-            else:
-                scale_on_scalar(rh_result[:], rh_result[:], m)
-            nc.sync.dma_start(out=out[m * P : (m + 1) * P, I:C], in_=rh_result[:])
-            if 1 <= m < LATE:
-                quantise_x(late[m], x_grouped)
-                for n in range(M_TILES):
-                    multiply(late[m], n, 0)
-            if m + 1 < LATE:
-                x_grouped = regroup_late(m + 1)
+            multiply(c7, m, 0)
+        rh_out(scale_on_vector, 2)
+        rh_out(scale_on_scalar, 3)
         scale_on_scalar(partial[:], partial[:], M_TILES - 1)
 
         for m in range(M_TILES):

from contextlib import ExitStack

import concourse.mybir as mybir
from concourse.masks import make_identity

F32 = mybir.dt.float32
BF16 = mybir.dt.bfloat16
U32 = mybir.dt.uint32
U8 = mybir.dt.uint8
I32 = mybir.dt.int32
E4M3_X4 = mybir.dt.float8_e4m3fn_x4
E5M2_X4 = mybir.dt.float8_e5m2_x4
ALU = mybir.AluOpType
ACT = mybir.ActivationFunctionType

B, I, H = 4096, 256, 512
C = I + H
P = 128
PACK = 4
K_PASS = P * PACK
PASSES = B // K_PASS
M_TILES = H // P
N_PASS = 512
HID_ROWS = (4, 4, 4, 4, 4, 4, 4, 2, 1, 1)
LATE = 3
EARLY = PASSES - LATE
GU_CUT = 320
X_LEAD = 2
X_CUT = 160
DENSE_LOADS = 5
DENSE_COLS = 32
GATE_COLS = 72
NO_SIGNS = 0x7FFF7FFF

FLOPS = 2 * B * H * C
BYTES = 2 * (B * I + 4 * B * H + 2 * H + 1) + 4 * H * C


def regroup(copy, grouped, rows):
    copy(
        out=grouped.rearrange("p (c i) t -> p c t i", i=4),
        in_=rows.rearrange("p t (c i) -> p c t i", i=4),
    )


def tile_persistentgrucell_pb_t_kernel(
    tc,
    x,
    rh,
    update,
    hidden,
    Wn,
    bn,
    connection_strength,
    connection_decay,
    connection_history,
    grad_out,
    out,
):
    nc = tc.nc
    with ExitStack() as ctx:
        ctx.enter_context(tc.manual_schedule())
        consts = ctx.enter_context(tc.tile_pool(name="consts", bufs=1))
        hid = ctx.enter_context(tc.tile_pool(name="hid", bufs=1))
        raw = ctx.enter_context(tc.tile_pool(name="raw", bufs=5))
        work = ctx.enter_context(tc.tile_pool(name="work", bufs=3))
        mx = ctx.enter_context(tc.tile_pool(name="mx", bufs=PASSES))
        results = ctx.enter_context(tc.tile_pool(name="results", bufs=M_TILES))
        psum = ctx.enter_context(tc.psum_pool(name="psum", bufs=1))

        warm = consts.tile([P, 1], F32)
        nc.vector.memset(warm[:], 0.0)
        nc.scalar.activation(out=warm[:], in_=warm[:], func=ACT.Sigmoid)

        vec_rows = consts.tile([P, P], BF16)
        nc.vector.memset(vec_rows[:], 0.0)
        nc.scalar.dma_start(
            out=vec_rows[0:M_TILES, :], in_=connection_history.rearrange("(m j) -> m j", j=P)
        )
        nc.scalar.dma_start(
            out=vec_rows[M_TILES : 2 * M_TILES, :],
            in_=connection_strength.rearrange("(m j) -> m j", j=P),
        )
        identity = consts.tile([P, P], BF16)
        make_identity(nc, identity[:])

        decay_bf16 = consts.tile([M_TILES, 1], BF16)
        nc.scalar.dma_start(out=decay_bf16[:], in_=connection_decay.partition_broadcast(M_TILES))

        pick = consts.tile([P, M_TILES, GATE_COLS], BF16)
        nc.vector.memset(pick[:], 0.0)
        for m in range(M_TILES):
            nc.vector.memset(pick[:, m, m : m + 1], 1.0 / B)

        hidden_rows = hidden.rearrange("(p r) j -> p r j", p=P)
        LAST = (M_TILES - 1, 0)
        spread = consts.tile([P, GATE_COLS], BF16)
        gate = consts.tile([P, M_TILES], F32)
        cs = consts.tile([P, M_TILES], F32)

        def make_spread():
            decay = consts.tile([M_TILES, 1], F32)
            nc.vector.tensor_copy(out=decay[:], in_=decay_bf16[:])
            nc.vector.tensor_copy(out=spread[:], in_=identity[:, 0:GATE_COLS])
            nc.vector.tensor_scalar_mul(
                out=spread[0:M_TILES, 0:M_TILES], in0=identity[0:M_TILES, 0:M_TILES], scalar1=decay[:, 0:1]
            )

        g_passes = grad_out.rearrange("(c p t) j -> c p t j", p=P, t=PACK)
        u_passes = update.rearrange("(c p t) j -> c p t j", p=P, t=PACK)
        rh_passes = rh.rearrange("(c p t) j -> c p t j", p=P, t=PACK)
        x_passes = x.rearrange("(c p t) j -> c p t j", p=P, t=PACK)

        windows = (slice(0, N_PASS), slice(C - N_PASS, C))
        acc = {}
        for m in range(M_TILES):
            for n in range(2):
                acc[(m, n)] = psum.tile([P, N_PASS], F32, name="acc%d%d" % (m, n), tag="acc%d%d" % (m, n))
        codes = {}

        def multiply(c, m, n):
            gu_codes, gu_scales, xr_codes, xr_scales = codes[c]
            nc.tensor.matmul_mx(
                out=acc[(m, n)][:],
                lhsT=gu_codes[:, m * P : (m + 1) * P].bitcast(E5M2_X4),
                lhsT_scale=gu_scales[:, m * P : (m + 1) * P],
                rhs=xr_codes[:, windows[n]].bitcast(E4M3_X4),
                rhs_scale=xr_scales[:, windows[n]],
                start=(c == 0 or (c == EARLY and (m, n) == LAST)),
                stop=(c == PASSES - 1 or (c == EARLY - 1 and (m, n) == LAST)),
            )

        def regroup_x(copy, c, x_raw):
            x_grouped = work.tile([P, I, PACK], BF16, name="x_grouped", align_bytes=64)
            regroup(copy, x_grouped[:], x_raw[:])
            return x_grouped

        def quantise_x(c, x_grouped):
            nc.vector.quantize_mx(
                out=codes[c][2][:, 0:I].bitcast(E4M3_X4),
                scales=codes[c][3][:, 0:I],
                in_=x_grouped[:].rearrange("p w t -> p (w t)"),
            )

        def load_x(c):
            x_raw = raw.tile([P, PACK, I], BF16, name="x_raw")
            nc.sync.dma_start(out=x_raw[:], in_=x_passes[c])
            return x_raw

        hid_raws = []
        x_raws = {}
        partial = consts.tile([P, I], F32)
        gates = []

        def load_hidden_and_late_x():
            first_row = 0
            for h, rows in enumerate(HID_ROWS):
                hid_raw = hid.tile([P, rows, H], BF16, name="hid_raw%d" % h)
                nc.sync.dma_start(out=hid_raw[:], in_=hidden_rows[:, first_row : first_row + rows, :])
                hid_raws.append(hid_raw)
                first_row += rows
                if h == len(HID_ROWS) - 1 - X_LEAD:
                    x_raws[EARLY] = load_x(EARLY)
            for c in range(EARLY + 1, PASSES):
                x_raws[c] = load_x(c)

        def open_gate():
            nc.scalar.copy(out=partial[:], in_=acc[LAST][:, 0:I])
            gate_psum = psum.tile([P, GATE_COLS], F32, name="gate_psum", tag="acc%d%d" % LAST)
            nc.tensor.matmul(out=gate_psum[:], lhsT=vec_rows[:], rhs=spread[:], start=True, stop=False)
            gates.append(gate_psum)

        def clear_signs(part):
            words = part.rearrange("p r j -> p (r j)").bitcast(I32)
            nc.vector.tensor_scalar(out=words, in0=words, scalar1=NO_SIGNS, scalar2=None, op0=ALU.bitwise_and)

        def absolute(part):
            nc.scalar.activation(out=part, in_=part, func=ACT.Abs)

        def gate_sums(h):
            cols = DENSE_COLS if h < DENSE_LOADS else GATE_COLS
            for r in range(HID_ROWS[h]):
                for m in range(M_TILES):
                    nc.tensor.matmul(
                        out=gates[0][:, 0:cols],
                        lhsT=hid_raws[h][:, r, m * P : (m + 1) * P],
                        rhs=pick[:, m, 0:cols],
                        start=False,
                        stop=(h == len(HID_ROWS) - 1 and r == HID_ROWS[h] - 1 and m == M_TILES - 1),
                    )

        def one_pass(c):
            rh_raw = raw.tile([P, PACK, H], BF16, name="rh_raw")
            g_raw = raw.tile([P, PACK, H], BF16, name="g_raw")
            u_raw = raw.tile([P, PACK, H], BF16, name="u_raw")
            if c == 0:
                nc.sync.dma_start(out=g_raw[:], in_=g_passes[c])
                nc.sync.dma_start(out=u_raw[:], in_=u_passes[c])
                nc.sync.dma_start(out=rh_raw[:], in_=rh_passes[c])
                x_raw = load_x(c)
            else:
                nc.sync.dma_start(out=rh_raw[:], in_=rh_passes[c])
                if c < EARLY:
                    x_raw = load_x(c)
                nc.sync.dma_start(out=g_raw[:], in_=g_passes[c])
                nc.sync.dma_start(out=u_raw[:], in_=u_passes[c])

            if c == PASSES - 1:
                load_hidden_and_late_x()
                open_gate()

            rh_grouped = work.tile([P, H, PACK], BF16, name="rh_grouped", align_bytes=64)
            regroup(nc.scalar.copy, rh_grouped[:], rh_raw[:])
            if c < EARLY:
                x_grouped = regroup_x(nc.scalar.copy, c, x_raw)

            gu_codes = mx.tile([P, H], U32, name="gu_codes", align_bytes=64)
            gu_scales = mx.tile([P, H], U8, name="gu_scales", align_bytes=64)
            xr_codes = mx.tile([P, C], U32, name="xr_codes", align_bytes=64)
            xr_scales = mx.tile([P, C], U8, name="xr_scales", align_bytes=64)
            codes[c] = (gu_codes, gu_scales, xr_codes, xr_scales)

            gu_rows = work.tile([P, PACK, H], BF16, name="gu_rows")
            gu_grouped = work.tile([P, H, PACK], BF16, name="gu_grouped", align_bytes=64)

            def quantise_rh():
                nc.vector.quantize_mx(
                    out=xr_codes[:, I:C].bitcast(E4M3_X4),
                    scales=xr_scales[:, I:C],
                    in_=rh_grouped[:].rearrange("p w t -> p (w t)"),
                )

            def quantise_gu():
                nc.vector.quantize_mx(
                    out=gu_codes[:].bitcast(E5M2_X4),
                    scales=gu_scales[:],
                    in_=gu_grouped[:].rearrange("p w t -> p (w t)"),
                )

            nc.vector.tensor_mul(out=gu_rows[:], in0=g_raw[:], in1=u_raw[:])
            if c == PASSES - 1:
                clear_signs(hid_raws[0][:])
                gate_sums(0)
            if c == 0:
                make_spread()
                regroup(nc.vector.tensor_copy, gu_grouped[:], gu_rows[:])
                quantise_gu()
                quantise_rh()
                quantise_x(c, x_grouped)
            else:
                quantise_rh()
                if c < EARLY:
                    regroup(nc.vector.tensor_copy, gu_grouped[:], gu_rows[:])
                    quantise_x(c, x_grouped)
                else:
                    regroup(nc.vector.tensor_copy, gu_grouped[:, 0:GU_CUT, :], gu_rows[:, :, 0:GU_CUT])
                    regroup(nc.scalar.copy, gu_grouped[:, GU_CUT:H, :], gu_rows[:, :, GU_CUT:H])
                quantise_gu()

        def products(c):
            for m in range(M_TILES):
                for n in range(2):
                    if n == 1 or c < EARLY:
                        multiply(c, m, n)

        for c in range(PASSES):
            one_pass(c)
            products(c)

        absolute(hid_raws[1][:])
        rh_results = []
        for m in range(M_TILES):
            rh_result = results.tile([P, H], F32, name="rh_result")
            nc.scalar.copy(out=rh_result[:], in_=acc[(m, 1)][:])
            rh_results.append(rh_result)

        x_grouped = {}

        def regroup_on_vector(c):
            x_grouped[c] = work.tile([P, I, PACK], BF16, name="x_grouped", align_bytes=64)
            regroup(nc.vector.tensor_copy, x_grouped[c][:, 0:X_CUT, :], x_raws[c][:, :, 0:X_CUT])

        def regroup_on_scalar(c):
            regroup(nc.scalar.copy, x_grouped[c][:, X_CUT:I, :], x_raws[c][:, :, X_CUT:I])

        def scale_on_scalar(dst, src, m):
            nc.scalar.activation(out=dst, in_=src, func=ACT.Copy, scale=cs[:, m : m + 1])

        def scale_on_vector(dst, src, m):
            nc.vector.tensor_scalar_mul(out=dst, in0=src, scalar1=cs[:, m : m + 1])

        def rh_out(scale, m):
            scale(rh_results[m][:], rh_results[m][:], m)
            nc.sync.dma_start(out=out[m * P : (m + 1) * P, I:C], in_=rh_results[m][:])

        c5, c6, c7 = range(EARLY, PASSES)
        for h in range(1, len(HID_ROWS)):
            if h == len(HID_ROWS) - X_LEAD:
                regroup_on_vector(c5)
                regroup_on_scalar(c5)
            if h > 1:
                clear_signs(hid_raws[h][:])
            gate_sums(h)
        gate_psum = gates[0]
        quantise_x(c5, x_grouped[c5])
        for m in range(M_TILES - 1):
            multiply(c5, m, 0)
        regroup_on_vector(c6)
        nc.scalar.activation(out=gate[:], in_=gate_psum[:, 0:M_TILES], func=ACT.Sigmoid)
        nc.vector.tensor_mul(out=cs[:], in0=gate[:], in1=gate_psum[:, M_TILES : 2 * M_TILES])
        acc[LAST] = psum.tile([P, N_PASS], F32, name="acc%d%d" % LAST, tag="acc%d%d" % LAST)
        regroup_on_scalar(c6)
        rh_out(scale_on_vector, 0)
        quantise_x(c6, x_grouped[c6])
        for m in range(M_TILES - 1):
            multiply(c6, m, 0)
        multiply(c5, *LAST)
        multiply(c6, *LAST)
        regroup_on_vector(c7)
        regroup_on_scalar(c7)
        rh_out(scale_on_scalar, 1)
        quantise_x(c7, x_grouped[c7])
        for m in range(M_TILES):
            multiply(c7, m, 0)
        rh_out(scale_on_vector, 2)
        rh_out(scale_on_scalar, 3)
        scale_on_scalar(partial[:], partial[:], M_TILES - 1)

        for m in range(M_TILES):
            x_result = results.tile([P, I], F32, name="x_result")
            if m == M_TILES - 1:
                nc.vector.scalar_tensor_tensor(
                    out=x_result[:],
                    in0=acc[LAST][:, 0:I],
                    scalar=cs[:, m : m + 1],
                    in1=partial[:],
                    op0=ALU.mult,
                    op1=ALU.add,
                )
            elif m % 2 == 0:
                scale_on_scalar(x_result[:], acc[(m, 0)][:, 0:I], m)
            else:
                scale_on_vector(x_result[:], acc[(m, 0)][:, 0:I], m)
            nc.sync.dma_start(out=out[m * P : (m + 1) * P, 0:I], in_=x_result[:])
